import numpy as np
import ml_dtypes


def mxq(x, axis, fmt="e4m3"):
    dtype, down = {"e4m3": (ml_dtypes.float8_e4m3fn, 7), "e5m2": (ml_dtypes.float8_e5m2, 14)}[fmt]
    v = np.moveaxis(np.asarray(x, np.float32).astype(ml_dtypes.bfloat16).astype(np.float64), axis, -1)
    blocks = v.reshape(v.shape[:-1] + (-1, 32))
    amax = np.abs(blocks).max(-1, keepdims=True)
    byte = np.maximum(np.where(amax > 0, np.frexp(amax)[1] - 1 + 127, 0) - down, 1)
    scale = np.exp2(byte - 127.0)
    codes = (blocks / scale).astype(np.float32).astype(dtype).astype(np.float64)
    return np.moveaxis((codes * scale).reshape(v.shape), -1, axis)


WIDE = False


def mx_kscale(k):
    if not WIDE:
        return np.ones(k)
    levels = np.array([10, -10, 5, -5, 0])
    a = np.random.permutation(np.resize(levels, k // 512 * 4)).reshape(k // 512, 4)
    idx = np.arange(k)
    return np.exp2(a[idx // 512, idx % 128 // 32])


BF16 = ml_dtypes.bfloat16


def bf(x):
    return np.asarray(x, np.float32).astype(BF16)


def f64(x):
    return np.asarray(x).astype(np.float64)


E2M1 = np.array([0.0, 0.5, 1.0, 1.5, 2.0, 3.0, 4.0, 6.0, -0.0, -0.5, -1.0, -1.5, -2.0, -3.0, -4.0, -6.0])


def pack_weight(w, fmt):
    k, n = w.shape
    w = f64(bf(w)).reshape(k // 32, 32, n)
    amax = np.abs(w).max(1)
    if fmt == "e4m3":
        byte = np.frexp(amax)[1] - 1 + 127 - 7
    else:
        mant, ex = np.frexp(amax / 6.0)
        byte = np.where(mant > 0.5, ex, ex - 1) + 127
    byte = np.clip(np.where(amax > 0, byte, 1), 1, 254)
    scaled = (w * np.exp2(127.0 - byte)[:, None, :]).reshape(k, n).astype(np.float32)
    by_word = np.ascontiguousarray(scaled.reshape(k // 512, 128, 4, n).transpose(0, 1, 3, 2))
    if fmt == "e4m3":
        words = by_word.astype(ml_dtypes.float8_e4m3fn).view(np.uint8)
    else:
        c = by_word.astype(ml_dtypes.float4_e2m1fn).view(np.uint8) & 0xF
        words = c[..., 0::2] | (c[..., 1::2] << 4)
    return np.ascontiguousarray(words), np.ascontiguousarray(byte.astype(np.uint8).reshape(k // 512, 16, n))


def unpack_weight(words, scales, fmt):
    g, p, n, _ = words.shape
    if fmt == "e4m3":
        vals = np.ascontiguousarray(words).view(ml_dtypes.float8_e4m3fn).astype(np.float64)
    else:
        nib = np.empty((g, p, n, 4), np.uint8)
        nib[..., 0::2] = words & 0xF
        nib[..., 1::2] = words >> 4
        vals = E2M1[nib]
    vals = vals * np.repeat(np.exp2(scales.astype(np.float64) - 127.0), 8, axis=1)[..., None]
    return vals.transpose(0, 1, 3, 2).reshape(g * 512, n)

def pack4(w):
    words, scales = pack_weight(w, "e2m1")
    return words.reshape(words.shape[0], 128, -1), scales


def unpack4(words, scales):
    return unpack_weight(words.reshape(words.shape[0], 128, -1, 2), scales, "e2m1")


N, IN, HID, OUT, MLP, NF = 256, 256, 512, 8192, 512, 8
FS = N // NF
G = 3 * HID


def sigmoid(v):
    return 1.0 / (1.0 + np.exp(-v))


def draw_hiddens():
    amp = 0.2 + 0.8 * np.random.random((N, 1))
    centre = np.repeat(np.random.standard_normal((NF, HID)), FS, axis=0)
    return amp * np.random.standard_normal((N, HID)) + 0.3 * centre


def setup_inputs():
    s = mx_kscale(OUT)
    ag_diff = bf(np.random.standard_normal((N, OUT)) * 2.0 * s)
    tension = bf(2.5 + 3.5 * np.random.random((N, 1)))
    hiddens = bf(draw_hiddens())
    W_io = np.random.standard_normal((G, OUT)) * 0.4 / np.sqrt(OUT) / s
    W_io_words, W_io_scales = pack4(np.ascontiguousarray(W_io.T))
    w_it = bf(np.random.standard_normal(G) * 0.1)
    W_hh = np.random.standard_normal((G, HID)) / np.sqrt(HID)
    W_hh_words, W_hh_scales = pack4(np.ascontiguousarray(W_hh.T))
    b_ih = bf(np.random.standard_normal(G) * 0.1)
    b_hh = bf(np.random.standard_normal(G) * 0.1)
    return {
        "ag_diff": ag_diff,
        "tension": tension,
        "hiddens": hiddens,
        "W_io_words": W_io_words,
        "W_io_scales": W_io_scales,
        "w_it": w_it,
        "W_hh_words": W_hh_words,
        "W_hh_scales": W_hh_scales,
        "b_ih": b_ih,
        "b_hh": b_hh,
    }


def reference(ag_diff, tension, hiddens, W_io_words, W_io_scales, w_it, W_hh_words, W_hh_scales, b_ih, b_hh):
    h = f64(hiddens)
    gi = (mxq(f64(ag_diff), 1, "e4m3") @ unpack4(W_io_words, W_io_scales)) + f64(tension) * f64(w_it) + f64(b_ih)
    gh = (mxq(h, 1, "e4m3") @ unpack4(W_hh_words, W_hh_scales)) + f64(b_hh)
    i_r, i_z, i_n = np.split(gi, 3, axis=-1)
    h_r, h_z, h_n = np.split(gh, 3, axis=-1)
    r = sigmoid(i_r + h_r)
    z = sigmoid(i_z + h_z)
    n = np.tanh(i_n + r * h_n)
    new_h = (1.0 - z) * n + z * h
    nh = new_h.reshape(NF, FS, HID)
    fmean = nh.mean(axis=1, keepdims=True)
    return (0.85 * nh + 0.15 * fmean).reshape(N, HID)

@@ -1,0 +1,223 @@
+from contextlib import ExitStack
+
+import concourse.mybir as mybir
+from concourse.masks import make_identity
+
+F32 = mybir.dt.float32
+BF16 = mybir.dt.bfloat16
+I32 = mybir.dt.int32
+U32 = mybir.dt.uint32
+U8 = mybir.dt.uint8
+FP8X4 = mybir.dt.float8_e4m3fn_x4
+FP4X4 = mybir.dt.float4_e2m1fn_x4
+ALU = mybir.AluOpType
+ACT = mybir.ActivationFunctionType
+
+P = 128
+K_PASS = 512
+CELLS = 256
+ROW_TILES = CELLS // P
+K_IN = 8192
+HID = 512
+FACTION = 32
+GATES = 3
+R_GATE, Z_GATE, N_GATE = 0, 1, 2
+GATE_COLS = GATES * HID
+IN_GROUPS = K_IN // K_PASS
+H_GROUP = IN_GROUPS
+GROUPS = IN_GROUPS + 1
+PSUM_BANKS = 8
+SCALE_ROWS = 16
+
+X_CHUNK_GROUPS = 4
+SCALE_RUN_GROUPS = 4
+K_TOGETHER = 12
+
+FLOPS = 2 * CELLS * (K_IN + HID) * GATE_COLS
+
+
+def tile_phiaslossengine_pb_k_kernel(
+    tc, ag_diff, tension, hiddens, W_io_words, W_io_scales, w_it, W_hh_words, W_hh_scales, b_ih, b_hh, out
+):
+    nc = tc.nc
+    with ExitStack() as stack:
+        stack.enter_context(tc.manual_schedule())
+        keep = stack.enter_context(tc.tile_pool(name="keep", bufs=1))
+        stage = stack.enter_context(tc.tile_pool(name="stage", bufs=4))
+        work = stack.enter_context(tc.tile_pool(name="work", bufs=2))
+        psum = stack.enter_context(tc.psum_pool(name="psum", bufs=1))
+
+        banks_taken = []
+
+        def next_bank(shape, dtype, name):
+            tag = "bank%d" % (len(banks_taken) % PSUM_BANKS)
+            banks_taken.append(name)
+            return psum.tile(shape, dtype, tag=tag, name=name)
+
+        x_sb = keep.tile([P, ROW_TILES, K_IN], BF16)
+        h_sb = keep.tile([P, ROW_TILES, HID], BF16)
+        w_words = keep.tile([P, GROUPS, 2 * GATE_COLS], U8, align_bytes=64)
+        w_planes = keep.tile([P, GROUPS, GATE_COLS], U8, align_bytes=64)
+        a_words = keep.tile([P, GROUPS, CELLS], U32, align_bytes=64)
+        a_planes = keep.tile([P, GROUPS, CELLS], U8, align_bytes=64)
+        ident = keep.tile([P, P], F32)
+        blend = keep.tile([P, P], F32)
+        side_lhsT = keep.tile([P, CELLS], BF16)
+        side_rhs = keep.tile([P, (GATES + 1) * HID], BF16)
+
+        nc.vector.memset(side_lhsT[:], 1.0)
+        nc.vector.memset(side_rhs[:], 0.0)
+        make_identity(nc, ident[:])
+        nc.scalar.dma_start(out=side_lhsT[0:1, :], in_=tension.rearrange("n o -> o n"))
+        nc.scalar.dma_start(out=side_rhs[0:1, 0:GATE_COLS], in_=w_it.unsqueeze(0))
+        nc.scalar.dma_start(out=side_rhs[1:2, 0:GATE_COLS], in_=b_ih.unsqueeze(0))
+        nc.scalar.dma_start(out=side_rhs[2:3, 0 : 2 * HID], in_=b_hh[0 : 2 * HID].unsqueeze(0))
+        nc.scalar.dma_start(out=side_rhs[2:3, GATE_COLS:], in_=b_hh[2 * HID :].unsqueeze(0))
+        nc.vector.memset(w_planes[:].bitcast(I32), 0)
+        nc.gpsimd.memset(blend[:], 0.0)
+        for f in range(P // FACTION):
+            cells = slice(f * FACTION, (f + 1) * FACTION)
+            nc.gpsimd.memset(blend[cells, cells], 1.0)
+
+        x_rows = ag_diff.rearrange("(r p) k -> p r k", p=P)
+        x_chunk = X_CHUNK_GROUPS * K_PASS
+        for c in range(IN_GROUPS // X_CHUNK_GROUPS):
+            cols = slice(c * x_chunk, (c + 1) * x_chunk)
+            nc.sync.dma_start(out=x_sb[:, :, cols], in_=x_rows[:, :, cols])
+        nc.sync.dma_start(out=h_sb[:], in_=hiddens.rearrange("(r p) k -> p r k", p=P))
+
+        def load_scale_rows(planes, rows):
+            for q in range(SCALE_ROWS // 2):
+                first = 32 * (q // 4) + q % 4
+                nc.sync.dma_start(
+                    out=planes[first:P:64].bitcast(I32),
+                    in_=rows[:, q : SCALE_ROWS : SCALE_ROWS // 2, :].rearrange("g q n -> q g n").bitcast(I32),
+                )
+
+        def load_words(kg, words):
+            nc.sync.dma_start(out=w_words[:, kg, :].bitcast(I32), in_=words.bitcast(I32))
+
+        load_scale_rows(w_planes[:, H_GROUP:GROUPS, :], W_hh_scales)
+        for run in range(IN_GROUPS // SCALE_RUN_GROUPS):
+            run_groups = range(run * SCALE_RUN_GROUPS, (run + 1) * SCALE_RUN_GROUPS)
+            groups = slice(run_groups[0], run_groups[-1] + 1)
+            load_scale_rows(w_planes[:, groups, :], W_io_scales[groups])
+            if run == 0:
+                load_words(H_GROUP, W_hh_words[0])
+            for g in run_groups:
+                load_words(g, W_io_words[g])
+
+        def transpose_group(kg, source):
+            flipped = next_bank([P, ROW_TILES, 2, P], F32, "flipped%d" % kg)
+            for rt in range(ROW_TILES):
+                pairs = source[:, rt, :].bitcast(F32)
+                for u in range(2):
+                    nc.tensor.transpose(flipped[:, rt, u, :], pairs[:, u : K_PASS // 2 : 2], ident[:])
+            grouped = stage.tile([P, CELLS * 4], BF16, align_bytes=64)
+            copy = nc.vector.tensor_copy if kg % 4 == 3 else nc.scalar.copy
+            copy(
+                out=grouped[:].bitcast(F32).rearrange("p (r c u) -> p r c u", r=ROW_TILES, u=2),
+                in_=flipped[:].rearrange("p r u c -> p r c u"),
+            )
+            return grouped
+
+        def quantise_group(kg, grouped):
+            nc.vector.quantize_mx(out=a_words[:, kg, :].bitcast(FP8X4), scales=a_planes[:, kg, :], in_=grouped[:])
+
+        waiting = None
+        for kg in range(GROUPS):
+            if kg == H_GROUP:
+                source = h_sb[:]
+            else:
+                source = x_sb[:, :, kg * K_PASS : (kg + 1) * K_PASS]
+            grouped = transpose_group(kg, source)
+            if waiting is not None:
+                quantise_group(kg - 1, waiting)
+            waiting = grouped
+        quantise_group(GROUPS - 1, waiting)
+
+        side = {}
+        for blk in range(GATES + 1):
+            for rt in range(ROW_TILES):
+                side_ps = next_bank([P, HID], F32, "side_ps%d%d" % (blk, rt))
+                nc.tensor.matmul(
+                    side_ps[:],
+                    lhsT=side_lhsT[:, rt * P : (rt + 1) * P],
+                    rhs=side_rhs[:, blk * HID : (blk + 1) * HID],
+                    start=True,
+                    stop=True,
+                )
+                side[blk, rt] = keep.tile([P, HID], F32, name="side%d%d" % (blk, rt))
+                copy = nc.scalar.copy if rt == 0 else nc.vector.tensor_copy
+                copy(out=side[blk, rt][:], in_=side_ps[:])
+        nc.vector.tensor_scalar_mul(out=blend[:], in0=blend[:], scalar1=0.15 / FACTION)
+        nc.vector.scalar_tensor_tensor(
+            out=blend[:], in0=ident[:], scalar=0.85, in1=blend[:], op0=ALU.mult, op1=ALU.add
+        )
+
+        acc = {}
+        for blk in range(GATES):
+            for rt in range(ROW_TILES):
+                acc[blk, rt] = next_bank([P, HID], F32, "acc%d%d" % (blk, rt))
+        h_n_ps = [next_bank([P, HID], F32, "h_n_ps%d" % rt) for rt in range(ROW_TILES)]
+
+        def mx_pass(target, kg, blk, rt, start, stop):
+            cells = slice(rt * P, (rt + 1) * P)
+            nc.tensor.matmul_mx(
+                out=target[:],
+                lhsT=a_words[:, kg, cells].bitcast(FP8X4),
+                lhsT_scale=a_planes[:, kg, cells],
+                rhs=w_words[:, kg, blk * 2 * HID : (blk + 1) * 2 * HID].bitcast(FP4X4),
+                rhs_scale=w_planes[:, kg, blk * HID : (blk + 1) * HID],
+                start=start,
+                stop=stop,
+            )
+
+        k_order = [H_GROUP] + list(range(IN_GROUPS))
+        for kg in k_order[:K_TOGETHER]:
+            for blk in range(GATES):
+                for rt in range(ROW_TILES):
+                    if kg == H_GROUP and blk == N_GATE:
+                        mx_pass(h_n_ps[rt], kg, blk, rt, start=True, stop=True)
+                    else:
+                        first = 0 if blk == N_GATE else H_GROUP
+                        mx_pass(acc[blk, rt], kg, blk, rt, start=(kg == first), stop=False)
+
+        h_n = []
+        for rt in range(ROW_TILES):
+            h_n.append(keep.tile([P, HID], F32, name="h_n%d" % rt))
+            nc.vector.tensor_add(out=h_n[rt][:], in0=h_n_ps[rt][:], in1=side[GATES, rt][:])
+
+        new_h = []
+        for rt in range(ROW_TILES):
+            for blk in range(GATES):
+                for kg in k_order[K_TOGETHER:]:
+                    mx_pass(acc[blk, rt], kg, blk, rt, start=False, stop=(kg == k_order[-1]))
+
+            r = work.tile([P, HID], F32, name="r")
+            nc.vector.tensor_add(out=r[:], in0=acc[R_GATE, rt][:], in1=side[R_GATE, rt][:])
+            nc.scalar.activation(out=r[:], in_=r[:], func=ACT.Sigmoid)
+            z_in = work.tile([P, HID], F32, name="z_in")
+            nc.vector.tensor_add(out=z_in[:], in0=acc[Z_GATE, rt][:], in1=side[Z_GATE, rt][:])
+            z = work.tile([P, HID], F32, name="z")
+            nc.scalar.activation(out=z[:], in_=z_in[:], func=ACT.Sigmoid)
+            one_minus_z = work.tile([P, HID], F32, name="one_minus_z")
+            nc.scalar.activation(out=one_minus_z[:], in_=z_in[:], func=ACT.Sigmoid, scale=-1.0)
+            n_rest = work.tile([P, HID], F32, name="n_rest")
+            nc.vector.tensor_mul(out=n_rest[:], in0=r[:], in1=h_n[rt][:])
+            nc.vector.tensor_add(out=n_rest[:], in0=n_rest[:], in1=side[N_GATE, rt][:])
+            n = work.tile([P, HID], F32, name="n")
+            nc.vector.tensor_add(out=n[:], in0=acc[N_GATE, rt][:], in1=n_rest[:])
+            nc.scalar.activation(out=n[:], in_=n[:], func=ACT.Tanh)
+            z_h = work.tile([P, HID], F32, name="z_h")
+            nc.vector.tensor_mul(out=z_h[:], in0=z[:], in1=h_sb[:, rt, :])
+            new_h.append(work.tile([P, HID], F32, name="new_h"))
+            nc.vector.tensor_mul(out=new_h[rt][:], in0=one_minus_z[:], in1=n[:])
+            nc.vector.tensor_add(out=new_h[rt][:], in0=new_h[rt][:], in1=z_h[:])
+
+        for rt in range(ROW_TILES):
+            out_ps = next_bank([P, HID], F32, "out_ps%d" % rt)
+            nc.tensor.matmul(out_ps[:], lhsT=blend[:], rhs=new_h[rt][:], start=True, stop=True)
+            out_sb = work.tile([P, HID], F32, name="out_sb")
+            nc.scalar.copy(out=out_sb[:], in_=out_ps[:])
+            nc.sync.dma_start(out=out[rt * P : (rt + 1) * P, :], in_=out_sb[:])

@@ -31,7 +31,8 @@ SCALE_ROWS = 16
 
 X_CHUNK_GROUPS = 4
 SCALE_RUN_GROUPS = 4
-K_TOGETHER = 12
+K_TOGETHER = 8
+HALF = HID // 2
 
 FLOPS = 2 * CELLS * (K_IN + HID) * GATE_COLS
 
@@ -54,10 +55,17 @@ def tile_phiaslossengine_pb_k_kernel(
             banks_taken.append(name)
             return psum.tile(shape, dtype, tag=tag, name=name)
 
-        x_sb = keep.tile([P, ROW_TILES, K_IN], BF16)
+        x_chunk = X_CHUNK_GROUPS * K_PASS
+        x_sb = [
+            keep.tile([P, ROW_TILES, x_chunk], BF16, name="x_sb%d" % c) for c in range(IN_GROUPS // X_CHUNK_GROUPS)
+        ]
         h_sb = keep.tile([P, ROW_TILES, HID], BF16)
-        w_words = keep.tile([P, GROUPS, 2 * GATE_COLS], U8, align_bytes=64)
-        w_planes = keep.tile([P, GROUPS, GATE_COLS], U8, align_bytes=64)
+        w_words = [keep.tile([P, 2 * GATE_COLS], U8, align_bytes=64, name="w_words%d" % kg) for kg in range(GROUPS)]
+        io_planes = [
+            keep.tile([P, SCALE_RUN_GROUPS, GATE_COLS], U8, align_bytes=64, name="io_planes%d" % run)
+            for run in range(IN_GROUPS // SCALE_RUN_GROUPS)
+        ]
+        hh_planes = keep.tile([P, 1, GATE_COLS], U8, align_bytes=64)
         a_words = keep.tile([P, GROUPS, CELLS], U32, align_bytes=64)
         a_planes = keep.tile([P, GROUPS, CELLS], U8, align_bytes=64)
         ident = keep.tile([P, P], F32)
@@ -73,17 +81,17 @@ def tile_phiaslossengine_pb_k_kernel(
         nc.scalar.dma_start(out=side_rhs[1:2, 0:GATE_COLS], in_=b_ih.unsqueeze(0))
         nc.scalar.dma_start(out=side_rhs[2:3, 0 : 2 * HID], in_=b_hh[0 : 2 * HID].unsqueeze(0))
         nc.scalar.dma_start(out=side_rhs[2:3, GATE_COLS:], in_=b_hh[2 * HID :].unsqueeze(0))
-        nc.vector.memset(w_planes[:].bitcast(I32), 0)
+        nc.vector.memset(hh_planes[:].bitcast(I32), 0)
+        for planes in io_planes:
+            nc.vector.memset(planes[:].bitcast(I32), 0)
         nc.gpsimd.memset(blend[:], 0.0)
         for f in range(P // FACTION):
             cells = slice(f * FACTION, (f + 1) * FACTION)
             nc.gpsimd.memset(blend[cells, cells], 1.0)
 
         x_rows = ag_diff.rearrange("(r p) k -> p r k", p=P)
-        x_chunk = X_CHUNK_GROUPS * K_PASS
         for c in range(IN_GROUPS // X_CHUNK_GROUPS):
-            cols = slice(c * x_chunk, (c + 1) * x_chunk)
-            nc.sync.dma_start(out=x_sb[:, :, cols], in_=x_rows[:, :, cols])
+            nc.sync.dma_start(out=x_sb[c][:], in_=x_rows[:, :, c * x_chunk : (c + 1) * x_chunk])
         nc.sync.dma_start(out=h_sb[:], in_=hiddens.rearrange("(r p) k -> p r k", p=P))
 
         def load_scale_rows(planes, rows):
@@ -95,13 +103,12 @@ def tile_phiaslossengine_pb_k_kernel(
                 )
 
         def load_words(kg, words):
-            nc.sync.dma_start(out=w_words[:, kg, :].bitcast(I32), in_=words.bitcast(I32))
+            nc.sync.dma_start(out=w_words[kg][:].bitcast(I32), in_=words.bitcast(I32))
 
-        load_scale_rows(w_planes[:, H_GROUP:GROUPS, :], W_hh_scales)
+        load_scale_rows(hh_planes, W_hh_scales)
         for run in range(IN_GROUPS // SCALE_RUN_GROUPS):
             run_groups = range(run * SCALE_RUN_GROUPS, (run + 1) * SCALE_RUN_GROUPS)
-            groups = slice(run_groups[0], run_groups[-1] + 1)
-            load_scale_rows(w_planes[:, groups, :], W_io_scales[groups])
+            load_scale_rows(io_planes[run], W_io_scales[run_groups[0] : run_groups[-1] + 1])
             if run == 0:
                 load_words(H_GROUP, W_hh_words[0])
             for g in run_groups:
@@ -129,7 +136,8 @@ def tile_phiaslossengine_pb_k_kernel(
             if kg == H_GROUP:
                 source = h_sb[:]
             else:
-                source = x_sb[:, :, kg * K_PASS : (kg + 1) * K_PASS]
+                place = kg % X_CHUNK_GROUPS
+                source = x_sb[kg // X_CHUNK_GROUPS][:, :, place * K_PASS : (place + 1) * K_PASS]
             grouped = transpose_group(kg, source)
             if waiting is not None:
                 quantise_group(kg - 1, waiting)
@@ -163,12 +171,16 @@ def tile_phiaslossengine_pb_k_kernel(
 
         def mx_pass(target, kg, blk, rt, start, stop):
             cells = slice(rt * P, (rt + 1) * P)
+            if kg == H_GROUP:
+                plane = hh_planes[:, 0, :]
+            else:
+                plane = io_planes[kg // SCALE_RUN_GROUPS][:, kg % SCALE_RUN_GROUPS, :]
             nc.tensor.matmul_mx(
                 out=target[:],
                 lhsT=a_words[:, kg, cells].bitcast(FP8X4),
                 lhsT_scale=a_planes[:, kg, cells],
-                rhs=w_words[:, kg, blk * 2 * HID : (blk + 1) * 2 * HID].bitcast(FP4X4),
-                rhs_scale=w_planes[:, kg, blk * HID : (blk + 1) * HID],
+                rhs=w_words[kg][:, blk * 2 * HID : (blk + 1) * 2 * HID].bitcast(FP4X4),
+                rhs_scale=plane[:, blk * HID : (blk + 1) * HID],
                 start=start,
                 stop=stop,
             )
@@ -188,12 +200,17 @@ def tile_phiaslossengine_pb_k_kernel(
             h_n.append(keep.tile([P, HID], F32, name="h_n%d" % rt))
             nc.vector.tensor_add(out=h_n[rt][:], in0=h_n_ps[rt][:], in1=side[GATES, rt][:])
 
+        k_rest = k_order[K_TOGETHER:]
+        for kg in k_rest:
+            for blk in range(GATES):
+                mx_pass(acc[blk, 0], kg, blk, 0, start=False, stop=(kg == k_rest[-1]))
+        for blk in range(GATES):
+            for kg in k_rest:
+                mx_pass(acc[blk, 1], kg, blk, 1, start=False, stop=(kg == k_rest[-1]))
+
+        halves = [slice(0, HALF), slice(HALF, HID)]
         new_h = []
         for rt in range(ROW_TILES):
-            for blk in range(GATES):
-                for kg in k_order[K_TOGETHER:]:
-                    mx_pass(acc[blk, rt], kg, blk, rt, start=False, stop=(kg == k_order[-1]))
-
             r = work.tile([P, HID], F32, name="r")
             nc.vector.tensor_add(out=r[:], in0=acc[R_GATE, rt][:], in1=side[R_GATE, rt][:])
             nc.scalar.activation(out=r[:], in_=r[:], func=ACT.Sigmoid)
@@ -206,18 +223,22 @@ def tile_phiaslossengine_pb_k_kernel(
             n_rest = work.tile([P, HID], F32, name="n_rest")
             nc.vector.tensor_mul(out=n_rest[:], in0=r[:], in1=h_n[rt][:])
             nc.vector.tensor_add(out=n_rest[:], in0=n_rest[:], in1=side[N_GATE, rt][:])
-            n = work.tile([P, HID], F32, name="n")
-            nc.vector.tensor_add(out=n[:], in0=acc[N_GATE, rt][:], in1=n_rest[:])
-            nc.scalar.activation(out=n[:], in_=n[:], func=ACT.Tanh)
             z_h = work.tile([P, HID], F32, name="z_h")
-            nc.vector.tensor_mul(out=z_h[:], in0=z[:], in1=h_sb[:, rt, :])
+            nc.gpsimd.tensor_tensor(out=z_h[:], in0=z[:], in1=h_sb[:, rt, :], op=ALU.mult)
+            n = work.tile([P, HID], F32, name="n")
+            for cols in halves:
+                nc.vector.tensor_add(out=n[:, cols], in0=acc[N_GATE, rt][:, cols], in1=n_rest[:, cols])
+                nc.scalar.activation(out=n[:, cols], in_=n[:, cols], func=ACT.Tanh)
+            mixer = nc.gpsimd if rt == 0 else nc.vector
             new_h.append(work.tile([P, HID], F32, name="new_h"))
-            nc.vector.tensor_mul(out=new_h[rt][:], in0=one_minus_z[:], in1=n[:])
-            nc.vector.tensor_add(out=new_h[rt][:], in0=new_h[rt][:], in1=z_h[:])
+            for cols in halves:
+                mixer.tensor_tensor(out=new_h[rt][:, cols], in0=one_minus_z[:, cols], in1=n[:, cols], op=ALU.mult)
+                mixer.tensor_tensor(out=new_h[rt][:, cols], in0=new_h[rt][:, cols], in1=z_h[:, cols], op=ALU.add)
 
         for rt in range(ROW_TILES):
             out_ps = next_bank([P, HID], F32, "out_ps%d" % rt)
-            nc.tensor.matmul(out_ps[:], lhsT=blend[:], rhs=new_h[rt][:], start=True, stop=True)
             out_sb = work.tile([P, HID], F32, name="out_sb")
-            nc.scalar.copy(out=out_sb[:], in_=out_ps[:])
-            nc.sync.dma_start(out=out[rt * P : (rt + 1) * P, :], in_=out_sb[:])
+            for cols in halves:
+                nc.tensor.matmul(out_ps[:, cols], lhsT=blend[:], rhs=new_h[rt][:, cols], start=True, stop=True)
+                nc.scalar.copy(out=out_sb[:, cols], in_=out_ps[:, cols])
+                nc.sync.dma_start(out=out[rt * P : (rt + 1) * P, cols], in_=out_sb[:, cols])

@@ -15,6 +15,7 @@ ACT = mybir.ActivationFunctionType
 
 P = 128
 K_PASS = 512
+PAIRS = K_PASS // 2
 CELLS = 256
 ROW_TILES = CELLS // P
 K_IN = 8192
@@ -25,14 +26,14 @@ R_GATE, Z_GATE, N_GATE = 0, 1, 2
 GATE_COLS = GATES * HID
 IN_GROUPS = K_IN // K_PASS
 H_GROUP = IN_GROUPS
-GROUPS = IN_GROUPS + 1
 PSUM_BANKS = 8
 SCALE_ROWS = 16
 
 X_CHUNK_GROUPS = 4
-SCALE_RUN_GROUPS = 4
-K_TOGETHER = 8
+WORD_CHUNK_GROUPS = 4
+SCALE_RUN_GROUPS = 16
 HALF = HID // 2
+QUARTER = HID // 4
 
 FLOPS = 2 * CELLS * (K_IN + HID) * GATE_COLS
 
@@ -45,7 +46,6 @@ def tile_phiaslossengine_pb_k_kernel(
         stack.enter_context(tc.manual_schedule())
         keep = stack.enter_context(tc.tile_pool(name="keep", bufs=1))
         stage = stack.enter_context(tc.tile_pool(name="stage", bufs=4))
-        work = stack.enter_context(tc.tile_pool(name="work", bufs=2))
         psum = stack.enter_context(tc.psum_pool(name="psum", bufs=1))
 
         banks_taken = []
@@ -55,19 +55,33 @@ def tile_phiaslossengine_pb_k_kernel(
             banks_taken.append(name)
             return psum.tile(shape, dtype, tag=tag, name=name)
 
-        x_chunk = X_CHUNK_GROUPS * K_PASS
+        def per_row_tile(shape, dtype, name):
+            return [keep.tile(shape, dtype, name="%s%d" % (name, rt)) for rt in range(ROW_TILES)]
+
         x_sb = [
-            keep.tile([P, ROW_TILES, x_chunk], BF16, name="x_sb%d" % c) for c in range(IN_GROUPS // X_CHUNK_GROUPS)
+            per_row_tile([P, X_CHUNK_GROUPS * K_PASS], BF16, "x_sb%d_" % c) for c in range(IN_GROUPS // X_CHUNK_GROUPS)
         ]
         h_sb = keep.tile([P, ROW_TILES, HID], BF16)
-        w_words = [keep.tile([P, 2 * GATE_COLS], U8, align_bytes=64, name="w_words%d" % kg) for kg in range(GROUPS)]
-        io_planes = [
-            keep.tile([P, SCALE_RUN_GROUPS, GATE_COLS], U8, align_bytes=64, name="io_planes%d" % run)
-            for run in range(IN_GROUPS // SCALE_RUN_GROUPS)
+        io_words = [
+            [
+                keep.tile([P, WORD_CHUNK_GROUPS, 2 * HID], U8, align_bytes=64, name="io_words%d_%d" % (blk, j))
+                for j in range(IN_GROUPS // WORD_CHUNK_GROUPS)
+            ]
+            for blk in range(GATES)
         ]
+        io_planes = [
+            [
+                keep.tile([P, SCALE_RUN_GROUPS, HID], U8, align_bytes=64, name="io_planes%d_%d" % (blk, run))
+                for run in range(IN_GROUPS // SCALE_RUN_GROUPS)
+            ]
+            for blk in range(GATES)
+        ]
+        hh_words = keep.tile([P, 2 * GATE_COLS], U8, align_bytes=64)
         hh_planes = keep.tile([P, 1, GATE_COLS], U8, align_bytes=64)
-        a_words = keep.tile([P, GROUPS, CELLS], U32, align_bytes=64)
-        a_planes = keep.tile([P, GROUPS, CELLS], U8, align_bytes=64)
+        a_words = keep.tile([P, ROW_TILES, IN_GROUPS, P], U32, align_bytes=64)
+        a_planes = keep.tile([P, ROW_TILES, IN_GROUPS, P], U8, align_bytes=64)
+        h_words = keep.tile([P, ROW_TILES, P], U32, align_bytes=64)
+        h_planes = keep.tile([P, ROW_TILES, P], U8, align_bytes=64)
         ident = keep.tile([P, P], F32)
         blend = keep.tile([P, P], F32)
         side_lhsT = keep.tile([P, CELLS], BF16)
@@ -76,22 +90,26 @@ def tile_phiaslossengine_pb_k_kernel(
         nc.vector.memset(side_lhsT[:], 1.0)
         nc.vector.memset(side_rhs[:], 0.0)
         make_identity(nc, ident[:])
-        nc.scalar.dma_start(out=side_lhsT[0:1, :], in_=tension.rearrange("n o -> o n"))
-        nc.scalar.dma_start(out=side_rhs[0:1, 0:GATE_COLS], in_=w_it.unsqueeze(0))
-        nc.scalar.dma_start(out=side_rhs[1:2, 0:GATE_COLS], in_=b_ih.unsqueeze(0))
-        nc.scalar.dma_start(out=side_rhs[2:3, 0 : 2 * HID], in_=b_hh[0 : 2 * HID].unsqueeze(0))
-        nc.scalar.dma_start(out=side_rhs[2:3, GATE_COLS:], in_=b_hh[2 * HID :].unsqueeze(0))
+        nc.gpsimd.dma_start(out=side_lhsT[0:1, :], in_=tension.rearrange("n o -> o n"))
+        nc.gpsimd.dma_start(out=side_rhs[0:1, 0:GATE_COLS], in_=w_it.unsqueeze(0))
+        nc.gpsimd.dma_start(out=side_rhs[1:2, 0:GATE_COLS], in_=b_ih.unsqueeze(0))
+        nc.gpsimd.dma_start(out=side_rhs[2:3, 0 : 2 * HID], in_=b_hh[0 : 2 * HID].unsqueeze(0))
+        nc.gpsimd.dma_start(out=side_rhs[2:3, GATE_COLS:], in_=b_hh[2 * HID :].unsqueeze(0))
         nc.vector.memset(hh_planes[:].bitcast(I32), 0)
-        for planes in io_planes:
-            nc.vector.memset(planes[:].bitcast(I32), 0)
+        for blk in range(GATES):
+            for planes in io_planes[blk]:
+                nc.vector.memset(planes[:].bitcast(I32), 0)
         nc.gpsimd.memset(blend[:], 0.0)
         for f in range(P // FACTION):
             cells = slice(f * FACTION, (f + 1) * FACTION)
             nc.gpsimd.memset(blend[cells, cells], 1.0)
 
-        x_rows = ag_diff.rearrange("(r p) k -> p r k", p=P)
         for c in range(IN_GROUPS // X_CHUNK_GROUPS):
-            nc.sync.dma_start(out=x_sb[c][:], in_=x_rows[:, :, c * x_chunk : (c + 1) * x_chunk])
+            for rt in range(ROW_TILES):
+                nc.sync.dma_start(
+                    out=x_sb[c][rt][:],
+                    in_=ag_diff[rt * P : (rt + 1) * P, c * X_CHUNK_GROUPS * K_PASS : (c + 1) * X_CHUNK_GROUPS * K_PASS],
+                )
         nc.sync.dma_start(out=h_sb[:], in_=hiddens.rearrange("(r p) k -> p r k", p=P))
 
         def load_scale_rows(planes, rows):
@@ -102,52 +120,70 @@ def tile_phiaslossengine_pb_k_kernel(
                     in_=rows[:, q : SCALE_ROWS : SCALE_ROWS // 2, :].rearrange("g q n -> q g n").bitcast(I32),
                 )
 
-        def load_words(kg, words):
-            nc.sync.dma_start(out=w_words[kg][:].bitcast(I32), in_=words.bitcast(I32))
-
         load_scale_rows(hh_planes, W_hh_scales)
-        for run in range(IN_GROUPS // SCALE_RUN_GROUPS):
-            run_groups = range(run * SCALE_RUN_GROUPS, (run + 1) * SCALE_RUN_GROUPS)
-            load_scale_rows(io_planes[run], W_io_scales[run_groups[0] : run_groups[-1] + 1])
-            if run == 0:
-                load_words(H_GROUP, W_hh_words[0])
-            for g in run_groups:
-                load_words(g, W_io_words[g])
+        nc.sync.dma_start(out=hh_words[:].bitcast(I32), in_=W_hh_words[0].bitcast(I32))
+        chunks_in_run = SCALE_RUN_GROUPS // WORD_CHUNK_GROUPS
+        for blk in range(GATES):
+            for run in range(IN_GROUPS // SCALE_RUN_GROUPS):
+                load_scale_rows(
+                    io_planes[blk][run],
+                    W_io_scales[run * SCALE_RUN_GROUPS : (run + 1) * SCALE_RUN_GROUPS, :, blk * HID : (blk + 1) * HID],
+                )
+                for j in range(run * chunks_in_run, (run + 1) * chunks_in_run):
+                    words = W_io_words[
+                        j * WORD_CHUNK_GROUPS : (j + 1) * WORD_CHUNK_GROUPS, :, blk * 2 * HID : (blk + 1) * 2 * HID
+                    ]
+                    nc.sync.dma_start(
+                        out=io_words[blk][j][:].bitcast(I32), in_=words.rearrange("g p n -> p g n").bitcast(I32)
+                    )
 
-        def transpose_group(kg, source):
-            flipped = next_bank([P, ROW_TILES, 2, P], F32, "flipped%d" % kg)
+        units = []
+        for c in range(IN_GROUPS // X_CHUNK_GROUPS):
             for rt in range(ROW_TILES):
-                pairs = source[:, rt, :].bitcast(F32)
+                pairs = x_sb[c][rt][:].bitcast(F32)
+                for place in range(0, X_CHUNK_GROUPS, 2):
+                    g = c * X_CHUNK_GROUPS + place
+                    units.append(
+                        (
+                            [pairs[:, (place + i) * PAIRS : (place + i + 1) * PAIRS] for i in range(2)],
+                            a_words[:, rt, g : g + 2, :],
+                            a_planes[:, rt, g : g + 2, :],
+                        )
+                    )
+        units.append(([h_sb[:, rt, :].bitcast(F32) for rt in range(ROW_TILES)], h_words[:], h_planes[:]))
+
+        def transpose_unit(number, sources):
+            flipped = next_bank([P, 2, 2, P], F32, "flipped")
+            for s in range(2):
                 for u in range(2):
-                    nc.tensor.transpose(flipped[:, rt, u, :], pairs[:, u : K_PASS // 2 : 2], ident[:])
-            grouped = stage.tile([P, CELLS * 4], BF16, align_bytes=64)
-            copy = nc.vector.tensor_copy if kg % 4 == 3 else nc.scalar.copy
+                    nc.tensor.transpose(flipped[:, s, u, :], sources[s][:, u:PAIRS:2], ident[:])
+            grouped = stage.tile([P, 2 * P * 4], BF16, align_bytes=64)
+            copy = nc.vector.tensor_copy if number % 4 == 3 else nc.scalar.copy
             copy(
-                out=grouped[:].bitcast(F32).rearrange("p (r c u) -> p r c u", r=ROW_TILES, u=2),
-                in_=flipped[:].rearrange("p r u c -> p r c u"),
+                out=grouped[:].bitcast(F32).rearrange("p (s c u) -> p s c u", s=2, u=2),
+                in_=flipped[:].rearrange("p s u c -> p s c u"),
             )
             return grouped
 
-        def quantise_group(kg, grouped):
-            nc.vector.quantize_mx(out=a_words[:, kg, :].bitcast(FP8X4), scales=a_planes[:, kg, :], in_=grouped[:])
+        def quantise_unit(grouped, words, planes):
+            nc.vector.quantize_mx(
+                out=words.rearrange("p s c -> p (s c)").bitcast(FP8X4),
+                scales=planes.rearrange("p s c -> p (s c)"),
+                in_=grouped[:],
+            )
 
         waiting = None
-        for kg in range(GROUPS):
-            if kg == H_GROUP:
-                source = h_sb[:]
-            else:
-                place = kg % X_CHUNK_GROUPS
-                source = x_sb[kg // X_CHUNK_GROUPS][:, :, place * K_PASS : (place + 1) * K_PASS]
-            grouped = transpose_group(kg, source)
+        for number, (sources, words, planes) in enumerate(units):
+            grouped = transpose_unit(number, sources)
             if waiting is not None:
-                quantise_group(kg - 1, waiting)
-            waiting = grouped
-        quantise_group(GROUPS - 1, waiting)
+                quantise_unit(*waiting)
+            waiting = (grouped, words, planes)
+        quantise_unit(*waiting)
 
-        side = {}
+        side = [per_row_tile([P, HID], F32, "side%d_" % blk) for blk in range(GATES + 1)]
         for blk in range(GATES + 1):
             for rt in range(ROW_TILES):
-                side_ps = next_bank([P, HID], F32, "side_ps%d%d" % (blk, rt))
+                side_ps = next_bank([P, HID], F32, "side_ps")
                 nc.tensor.matmul(
                     side_ps[:],
                     lhsT=side_lhsT[:, rt * P : (rt + 1) * P],
@@ -155,90 +191,98 @@ def tile_phiaslossengine_pb_k_kernel(
                     start=True,
                     stop=True,
                 )
-                side[blk, rt] = keep.tile([P, HID], F32, name="side%d%d" % (blk, rt))
                 copy = nc.scalar.copy if rt == 0 else nc.vector.tensor_copy
-                copy(out=side[blk, rt][:], in_=side_ps[:])
+                copy(out=side[blk][rt][:], in_=side_ps[:])
         nc.vector.tensor_scalar_mul(out=blend[:], in0=blend[:], scalar1=0.15 / FACTION)
         nc.vector.scalar_tensor_tensor(
             out=blend[:], in0=ident[:], scalar=0.85, in1=blend[:], op0=ALU.mult, op1=ALU.add
         )
 
-        acc = {}
-        for blk in range(GATES):
-            for rt in range(ROW_TILES):
-                acc[blk, rt] = next_bank([P, HID], F32, "acc%d%d" % (blk, rt))
-        h_n_ps = [next_bank([P, HID], F32, "h_n_ps%d" % rt) for rt in range(ROW_TILES)]
-
-        def mx_pass(target, kg, blk, rt, start, stop):
-            cells = slice(rt * P, (rt + 1) * P)
+        def mx_pass(target, kg, rt, blk, first_col, width, start, stop):
             if kg == H_GROUP:
-                plane = hh_planes[:, 0, :]
+                lhsT, lhsT_scale = h_words[:, rt, :], h_planes[:, rt, :]
+                rhs = hh_words[:, blk * 2 * HID : (blk + 1) * 2 * HID]
+                rhs_scale = hh_planes[:, 0, blk * HID : (blk + 1) * HID]
             else:
-                plane = io_planes[kg // SCALE_RUN_GROUPS][:, kg % SCALE_RUN_GROUPS, :]
+                lhsT, lhsT_scale = a_words[:, rt, kg, :], a_planes[:, rt, kg, :]
+                rhs = io_words[blk][kg // WORD_CHUNK_GROUPS][:, kg % WORD_CHUNK_GROUPS, :]
+                rhs_scale = io_planes[blk][kg // SCALE_RUN_GROUPS][:, kg % SCALE_RUN_GROUPS, :]
             nc.tensor.matmul_mx(
-                out=target[:],
-                lhsT=a_words[:, kg, cells].bitcast(FP8X4),
-                lhsT_scale=a_planes[:, kg, cells],
-                rhs=w_words[kg][:, blk * 2 * HID : (blk + 1) * 2 * HID].bitcast(FP4X4),
-                rhs_scale=plane[:, blk * HID : (blk + 1) * HID],
+                out=target,
+                lhsT=lhsT.bitcast(FP8X4),
+                lhsT_scale=lhsT_scale,
+                rhs=rhs[:, 2 * first_col : 2 * (first_col + width)].bitcast(FP4X4),
+                rhs_scale=rhs_scale[:, first_col : first_col + width],
                 start=start,
                 stop=stop,
             )
 
-        k_order = [H_GROUP] + list(range(IN_GROUPS))
-        for kg in k_order[:K_TOGETHER]:
-            for blk in range(GATES):
+        h_n = per_row_tile([P, HID], F32, "h_n")
+        for rt in range(ROW_TILES):
+            h_n_ps = next_bank([P, HID], F32, "h_n_ps")
+            mx_pass(h_n_ps[:], H_GROUP, rt, N_GATE, 0, HID, start=True, stop=True)
+            nc.vector.tensor_add(out=h_n[rt][:], in0=h_n_ps[:], in1=side[GATES][rt][:])
+
+        def whole_gate(blk):
+            sums = [next_bank([P, HID], F32, "gate_sum") for rt in range(ROW_TILES)]
+            for kg in [H_GROUP] + list(range(IN_GROUPS)):
                 for rt in range(ROW_TILES):
-                    if kg == H_GROUP and blk == N_GATE:
-                        mx_pass(h_n_ps[rt], kg, blk, rt, start=True, stop=True)
-                    else:
-                        first = 0 if blk == N_GATE else H_GROUP
-                        mx_pass(acc[blk, rt], kg, blk, rt, start=(kg == first), stop=False)
+                    mx_pass(sums[rt][:], kg, rt, blk, 0, HID, start=(kg == H_GROUP), stop=(kg == IN_GROUPS - 1))
+            return sums
 
-        h_n = []
+        r = per_row_tile([P, HID], F32, "r")
+        n_rest = per_row_tile([P, HID], F32, "n_rest")
+        sums = whole_gate(R_GATE)
         for rt in range(ROW_TILES):
-            h_n.append(keep.tile([P, HID], F32, name="h_n%d" % rt))
-            nc.vector.tensor_add(out=h_n[rt][:], in0=h_n_ps[rt][:], in1=side[GATES, rt][:])
+            nc.vector.tensor_add(out=r[rt][:], in0=sums[rt][:], in1=side[R_GATE][rt][:])
+            nc.scalar.activation(out=r[rt][:], in_=r[rt][:], func=ACT.Sigmoid)
+        for rt in range(ROW_TILES):
+            nc.vector.tensor_mul(out=n_rest[rt][:], in0=r[rt][:], in1=h_n[rt][:])
+            nc.vector.tensor_add(out=n_rest[rt][:], in0=n_rest[rt][:], in1=side[N_GATE][rt][:])
 
-        k_rest = k_order[K_TOGETHER:]
-        for kg in k_rest:
-            for blk in range(GATES):
-                mx_pass(acc[blk, 0], kg, blk, 0, start=False, stop=(kg == k_rest[-1]))
-        for blk in range(GATES):
-            for kg in k_rest:
-                mx_pass(acc[blk, 1], kg, blk, 1, start=False, stop=(kg == k_rest[-1]))
+        z_in = per_row_tile([P, HID], F32, "z_in")
+        z = per_row_tile([P, HID], F32, "z")
+        one_minus_z = per_row_tile([P, HID], F32, "one_minus_z")
+        z_h = per_row_tile([P, HID], F32, "z_h")
+        sums = whole_gate(Z_GATE)
+        for rt in range(ROW_TILES):
+            nc.vector.tensor_add(out=z_in[rt][:], in0=sums[rt][:], in1=side[Z_GATE][rt][:])
+            nc.scalar.activation(out=z[rt][:], in_=z_in[rt][:], func=ACT.Sigmoid)
+            nc.scalar.activation(out=one_minus_z[rt][:], in_=z_in[rt][:], func=ACT.Sigmoid, scale=-1.0)
+        for rt in range(ROW_TILES):
+            nc.vector.tensor_mul(out=z_h[rt][:], in0=z[rt][:], in1=h_sb[:, rt, :])
 
+        n = per_row_tile([P, HID], F32, "n")
+        new_h = per_row_tile([P, HID], F32, "new_h")
+        out_sb = per_row_tile([P, HID], F32, "out_sb")
+
+        def mix(rt, cols, i_n, mixer):
+            nc.vector.tensor_add(out=n[rt][:, cols], in0=i_n, in1=n_rest[rt][:, cols])
+            nc.scalar.activation(out=n[rt][:, cols], in_=n[rt][:, cols], func=ACT.Tanh)
+            mixer.tensor_tensor(out=new_h[rt][:, cols], in0=one_minus_z[rt][:, cols], in1=n[rt][:, cols], op=ALU.mult)
+            mixer.tensor_tensor(out=new_h[rt][:, cols], in0=new_h[rt][:, cols], in1=z_h[rt][:, cols], op=ALU.add)
+
+        def smooth_and_store(rt, cols, width):
+            out_ps = next_bank([P, width], F32, "out_ps")
+            nc.tensor.matmul(out_ps[:], lhsT=blend[:], rhs=new_h[rt][:, cols], start=True, stop=True)
+            nc.scalar.copy(out=out_sb[rt][:, cols], in_=out_ps[:])
+            nc.sync.dma_start(out=out[rt * P : (rt + 1) * P, cols], in_=out_sb[rt][:, cols])
+
+        i_n = next_bank([P, HID], F32, "i_n")
+        for g in range(IN_GROUPS):
+            mx_pass(i_n[:], g, 0, N_GATE, 0, HID, start=(g == 0), stop=(g == IN_GROUPS - 1))
         halves = [slice(0, HALF), slice(HALF, HID)]
-        new_h = []
-        for rt in range(ROW_TILES):
-            r = work.tile([P, HID], F32, name="r")
-            nc.vector.tensor_add(out=r[:], in0=acc[R_GATE, rt][:], in1=side[R_GATE, rt][:])
-            nc.scalar.activation(out=r[:], in_=r[:], func=ACT.Sigmoid)
-            z_in = work.tile([P, HID], F32, name="z_in")
-            nc.vector.tensor_add(out=z_in[:], in0=acc[Z_GATE, rt][:], in1=side[Z_GATE, rt][:])
-            z = work.tile([P, HID], F32, name="z")
-            nc.scalar.activation(out=z[:], in_=z_in[:], func=ACT.Sigmoid)
-            one_minus_z = work.tile([P, HID], F32, name="one_minus_z")
-            nc.scalar.activation(out=one_minus_z[:], in_=z_in[:], func=ACT.Sigmoid, scale=-1.0)
-            n_rest = work.tile([P, HID], F32, name="n_rest")
-            nc.vector.tensor_mul(out=n_rest[:], in0=r[:], in1=h_n[rt][:])
-            nc.vector.tensor_add(out=n_rest[:], in0=n_rest[:], in1=side[N_GATE, rt][:])
-            z_h = work.tile([P, HID], F32, name="z_h")
-            nc.gpsimd.tensor_tensor(out=z_h[:], in0=z[:], in1=h_sb[:, rt, :], op=ALU.mult)
-            n = work.tile([P, HID], F32, name="n")
-            for cols in halves:
-                nc.vector.tensor_add(out=n[:, cols], in0=acc[N_GATE, rt][:, cols], in1=n_rest[:, cols])
-                nc.scalar.activation(out=n[:, cols], in_=n[:, cols], func=ACT.Tanh)
-            mixer = nc.gpsimd if rt == 0 else nc.vector
-            new_h.append(work.tile([P, HID], F32, name="new_h"))
-            for cols in halves:
-                mixer.tensor_tensor(out=new_h[rt][:, cols], in0=one_minus_z[:, cols], in1=n[:, cols], op=ALU.mult)
-                mixer.tensor_tensor(out=new_h[rt][:, cols], in0=new_h[rt][:, cols], in1=z_h[:, cols], op=ALU.add)
+        for cols in halves:
+            mix(0, cols, i_n[:, cols], nc.gpsimd)
 
-        for rt in range(ROW_TILES):
-            out_ps = next_bank([P, HID], F32, "out_ps%d" % rt)
-            out_sb = work.tile([P, HID], F32, name="out_sb")
-            for cols in halves:
-                nc.tensor.matmul(out_ps[:, cols], lhsT=blend[:], rhs=new_h[rt][:, cols], start=True, stop=True)
-                nc.scalar.copy(out=out_sb[:, cols], in_=out_ps[:, cols])
-                nc.sync.dma_start(out=out[rt * P : (rt + 1) * P, cols], in_=out_sb[:, cols])
+        quarters = [slice(q * QUARTER, (q + 1) * QUARTER) for q in range(HID // QUARTER)]
+        for q, cols in enumerate(quarters):
+            i_n = next_bank([P, QUARTER], F32, "i_n_quarter")
+            for g in range(IN_GROUPS):
+                mx_pass(i_n[:], g, 1, N_GATE, q * QUARTER, QUARTER, start=(g == 0), stop=(g == IN_GROUPS - 1))
+            mix(1, cols, i_n[:], nc.vector)
+            if q > 0:
+                smooth_and_store(1, quarters[q - 1], QUARTER)
+        for cols in halves:
+            smooth_and_store(0, cols, HALF)
+        smooth_and_store(1, quarters[-1], QUARTER)

@@ -29,9 +29,12 @@ H_GROUP = IN_GROUPS
 PSUM_BANKS = 8
 SCALE_ROWS = 16
 
-X_CHUNK_GROUPS = 4
-WORD_CHUNK_GROUPS = 4
-SCALE_RUN_GROUPS = 16
+UNIT_GROUPS = 2
+CHUNK_GROUPS = 4
+CHUNKS = IN_GROUPS // CHUNK_GROUPS
+RZ_WORD_GROUPS = 2
+N_WORD_GROUPS = 4
+HELD_BACK = 4
 HALF = HID // 2
 QUARTER = HID // 4
 
@@ -45,72 +48,51 @@ def tile_phiaslossengine_pb_k_kernel(
     with ExitStack() as stack:
         stack.enter_context(tc.manual_schedule())
         keep = stack.enter_context(tc.tile_pool(name="keep", bufs=1))
-        stage = stack.enter_context(tc.tile_pool(name="stage", bufs=4))
+        stage = stack.enter_context(tc.tile_pool(name="stage", bufs=5))
         psum = stack.enter_context(tc.psum_pool(name="psum", bufs=1))
 
-        banks_taken = []
-
-        def next_bank(shape, dtype, name):
-            tag = "bank%d" % (len(banks_taken) % PSUM_BANKS)
-            banks_taken.append(name)
-            return psum.tile(shape, dtype, tag=tag, name=name)
+        def bank(number, shape, dtype, name):
+            return psum.tile(shape, dtype, tag="bank%d" % number, name=name)
 
         def per_row_tile(shape, dtype, name):
             return [keep.tile(shape, dtype, name="%s%d" % (name, rt)) for rt in range(ROW_TILES)]
 
-        x_sb = [
-            per_row_tile([P, X_CHUNK_GROUPS * K_PASS], BF16, "x_sb%d_" % c) for c in range(IN_GROUPS // X_CHUNK_GROUPS)
-        ]
-        h_sb = keep.tile([P, ROW_TILES, HID], BF16)
-        io_words = [
-            [
-                keep.tile([P, WORD_CHUNK_GROUPS, 2 * HID], U8, align_bytes=64, name="io_words%d_%d" % (blk, j))
-                for j in range(IN_GROUPS // WORD_CHUNK_GROUPS)
-            ]
-            for blk in range(GATES)
-        ]
-        io_planes = [
-            [
-                keep.tile([P, SCALE_RUN_GROUPS, HID], U8, align_bytes=64, name="io_planes%d_%d" % (blk, run))
-                for run in range(IN_GROUPS // SCALE_RUN_GROUPS)
-            ]
-            for blk in range(GATES)
-        ]
-        hh_words = keep.tile([P, 2 * GATE_COLS], U8, align_bytes=64)
-        hh_planes = keep.tile([P, 1, GATE_COLS], U8, align_bytes=64)
-        a_words = keep.tile([P, ROW_TILES, IN_GROUPS, P], U32, align_bytes=64)
-        a_planes = keep.tile([P, ROW_TILES, IN_GROUPS, P], U8, align_bytes=64)
-        h_words = keep.tile([P, ROW_TILES, P], U32, align_bytes=64)
-        h_planes = keep.tile([P, ROW_TILES, P], U8, align_bytes=64)
-        ident = keep.tile([P, P], F32)
-        blend = keep.tile([P, P], F32)
         side_lhsT = keep.tile([P, CELLS], BF16)
         side_rhs = keep.tile([P, (GATES + 1) * HID], BF16)
-
+        table_warmer = keep.tile([P, 1], F32)
+        ident = keep.tile([P, P], F32)
+        blend = keep.tile([P, P], F32)
         nc.vector.memset(side_lhsT[:], 1.0)
         nc.vector.memset(side_rhs[:], 0.0)
+        nc.vector.memset(table_warmer[:], 0.0)
         make_identity(nc, ident[:])
-        nc.gpsimd.dma_start(out=side_lhsT[0:1, :], in_=tension.rearrange("n o -> o n"))
-        nc.gpsimd.dma_start(out=side_rhs[0:1, 0:GATE_COLS], in_=w_it.unsqueeze(0))
-        nc.gpsimd.dma_start(out=side_rhs[1:2, 0:GATE_COLS], in_=b_ih.unsqueeze(0))
-        nc.gpsimd.dma_start(out=side_rhs[2:3, 0 : 2 * HID], in_=b_hh[0 : 2 * HID].unsqueeze(0))
-        nc.gpsimd.dma_start(out=side_rhs[2:3, GATE_COLS:], in_=b_hh[2 * HID :].unsqueeze(0))
-        nc.vector.memset(hh_planes[:].bitcast(I32), 0)
-        for blk in range(GATES):
-            for planes in io_planes[blk]:
-                nc.vector.memset(planes[:].bitcast(I32), 0)
+        nc.scalar.dma_start(out=side_lhsT[0:1, :], in_=tension.rearrange("n o -> o n"))
+        nc.scalar.dma_start(out=side_rhs[0:1, 0:GATE_COLS], in_=w_it.unsqueeze(0))
+        nc.scalar.dma_start(out=side_rhs[1:2, 0:GATE_COLS], in_=b_ih.unsqueeze(0))
+        nc.scalar.dma_start(out=side_rhs[2:3, 0 : 2 * HID], in_=b_hh[0 : 2 * HID].unsqueeze(0))
+        nc.scalar.dma_start(out=side_rhs[2:3, GATE_COLS:], in_=b_hh[2 * HID :].unsqueeze(0))
+        nc.scalar.activation(out=table_warmer[:], in_=table_warmer[:], func=ACT.Sigmoid)
         nc.gpsimd.memset(blend[:], 0.0)
         for f in range(P // FACTION):
             cells = slice(f * FACTION, (f + 1) * FACTION)
             nc.gpsimd.memset(blend[cells, cells], 1.0)
 
-        for c in range(IN_GROUPS // X_CHUNK_GROUPS):
-            for rt in range(ROW_TILES):
-                nc.sync.dma_start(
-                    out=x_sb[c][rt][:],
-                    in_=ag_diff[rt * P : (rt + 1) * P, c * X_CHUNK_GROUPS * K_PASS : (c + 1) * X_CHUNK_GROUPS * K_PASS],
-                )
-        nc.sync.dma_start(out=h_sb[:], in_=hiddens.rearrange("(r p) k -> p r k", p=P))
+        x_pairs = {}
+
+        def load_x(first_group, groups, rt):
+            x_sb = keep.tile([P, groups * K_PASS], BF16, name="x_sb%d_%d" % (first_group, rt))
+            nc.sync.dma_start(
+                out=x_sb[:],
+                in_=ag_diff[rt * P : (rt + 1) * P, first_group * K_PASS : (first_group + groups) * K_PASS],
+            )
+            pairs = x_sb[:].bitcast(F32)
+            for place in range(0, groups, UNIT_GROUPS):
+                x_pairs[(first_group + place, rt)] = pairs[:, place * PAIRS : (place + UNIT_GROUPS) * PAIRS]
+
+        def new_planes(groups, columns, name):
+            planes = keep.tile([P, groups, columns], U8, align_bytes=64, name=name)
+            nc.vector.memset(planes[:].bitcast(I32), 0)
+            return planes
 
         def load_scale_rows(planes, rows):
             for q in range(SCALE_ROWS // 2):
@@ -120,70 +102,88 @@ def tile_phiaslossengine_pb_k_kernel(
                     in_=rows[:, q : SCALE_ROWS : SCALE_ROWS // 2, :].rearrange("g q n -> q g n").bitcast(I32),
                 )
 
-        load_scale_rows(hh_planes, W_hh_scales)
-        nc.sync.dma_start(out=hh_words[:].bitcast(I32), in_=W_hh_words[0].bitcast(I32))
-        chunks_in_run = SCALE_RUN_GROUPS // WORD_CHUNK_GROUPS
-        for blk in range(GATES):
-            for run in range(IN_GROUPS // SCALE_RUN_GROUPS):
-                load_scale_rows(
-                    io_planes[blk][run],
-                    W_io_scales[run * SCALE_RUN_GROUPS : (run + 1) * SCALE_RUN_GROUPS, :, blk * HID : (blk + 1) * HID],
-                )
-                for j in range(run * chunks_in_run, (run + 1) * chunks_in_run):
-                    words = W_io_words[
-                        j * WORD_CHUNK_GROUPS : (j + 1) * WORD_CHUNK_GROUPS, :, blk * 2 * HID : (blk + 1) * 2 * HID
-                    ]
-                    nc.sync.dma_start(
-                        out=io_words[blk][j][:].bitcast(I32), in_=words.rearrange("g p n -> p g n").bitcast(I32)
-                    )
+        def load_words(first_group, groups, first_byte, n_bytes, name):
+            words = keep.tile([P, groups, n_bytes], U8, align_bytes=64, name=name)
+            nc.sync.dma_start(
+                out=words[:].bitcast(I32),
+                in_=W_io_words[first_group : first_group + groups, :, first_byte : first_byte + n_bytes]
+                .rearrange("g p n -> p g n")
+                .bitcast(I32),
+            )
+            return words
 
-        units = []
-        for c in range(IN_GROUPS // X_CHUNK_GROUPS):
+        rz_planes = []
+        rz_words = []
+
+        def load_rz(c):
+            load_scale_rows(
+                rz_planes[c], W_io_scales[c * CHUNK_GROUPS : (c + 1) * CHUNK_GROUPS, :, 0 : 2 * HID]
+            )
+            for g in range(c * CHUNK_GROUPS, (c + 1) * CHUNK_GROUPS, RZ_WORD_GROUPS):
+                rz_words.append(load_words(g, RZ_WORD_GROUPS, 0, 4 * HID, "rz_words%d" % g))
+
+        h_sb = keep.tile([P, ROW_TILES, HID], BF16)
+        rz_planes.append(new_planes(CHUNK_GROUPS, 2 * HID, "rz_planes0"))
+        rz_planes.append(new_planes(CHUNK_GROUPS, 2 * HID, "rz_planes1"))
+        for g in range(0, CHUNK_GROUPS, UNIT_GROUPS):
             for rt in range(ROW_TILES):
-                pairs = x_sb[c][rt][:].bitcast(F32)
-                for place in range(0, X_CHUNK_GROUPS, 2):
-                    g = c * X_CHUNK_GROUPS + place
-                    units.append(
-                        (
-                            [pairs[:, (place + i) * PAIRS : (place + i + 1) * PAIRS] for i in range(2)],
-                            a_words[:, rt, g : g + 2, :],
-                            a_planes[:, rt, g : g + 2, :],
-                        )
-                    )
-        units.append(([h_sb[:, rt, :].bitcast(F32) for rt in range(ROW_TILES)], h_words[:], h_planes[:]))
+                load_x(g, UNIT_GROUPS, rt)
+        nc.sync.dma_start(out=h_sb[:], in_=hiddens.rearrange("(r p) k -> p r k", p=P))
+        load_rz(0)
+        for rt in range(ROW_TILES):
+            load_x(CHUNK_GROUPS, CHUNK_GROUPS, rt)
+        load_rz(1)
+        for rt in range(ROW_TILES):
+            load_x(2 * CHUNK_GROUPS, CHUNK_GROUPS, rt)
 
-        def transpose_unit(number, sources):
-            flipped = next_bank([P, 2, 2, P], F32, "flipped")
+        a_words = {}
+        a_planes = {}
+
+        def transpose_unit(number, sources, copy):
+            flipped = bank(number, [P, 2, 2, P], F32, "flipped")
             for s in range(2):
                 for u in range(2):
                     nc.tensor.transpose(flipped[:, s, u, :], sources[s][:, u:PAIRS:2], ident[:])
             grouped = stage.tile([P, 2 * P * 4], BF16, align_bytes=64)
-            copy = nc.vector.tensor_copy if number % 4 == 3 else nc.scalar.copy
             copy(
                 out=grouped[:].bitcast(F32).rearrange("p (s c u) -> p s c u", s=2, u=2),
                 in_=flipped[:].rearrange("p s u c -> p s c u"),
             )
             return grouped
 
-        def quantise_unit(grouped, words, planes):
+        def quantise_unit(key, label, grouped):
+            a_words[key] = keep.tile([P, 2, P], U32, align_bytes=64, name="a_words" + label)
+            a_planes[key] = keep.tile([P, 2, P], U8, align_bytes=64, name="a_planes" + label)
             nc.vector.quantize_mx(
-                out=words.rearrange("p s c -> p (s c)").bitcast(FP8X4),
-                scales=planes.rearrange("p s c -> p (s c)"),
+                out=a_words[key][:].rearrange("p s c -> p (s c)").bitcast(FP8X4),
+                scales=a_planes[key][:].rearrange("p s c -> p (s c)"),
                 in_=grouped[:],
             )
 
-        waiting = None
-        for number, (sources, words, planes) in enumerate(units):
-            grouped = transpose_unit(number, sources)
-            if waiting is not None:
-                quantise_unit(*waiting)
-            waiting = (grouped, words, planes)
-        quantise_unit(*waiting)
+        def transpose_run(c, with_hiddens):
+            units = []
+            for g in range(c * CHUNK_GROUPS, (c + 1) * CHUNK_GROUPS, UNIT_GROUPS):
+                for rt in range(ROW_TILES):
+                    pairs = x_pairs[(g, rt)]
+                    units.append(((g, rt), "%d_%d" % (g, rt), [pairs[:, 0:PAIRS], pairs[:, PAIRS : 2 * PAIRS]]))
+            if with_hiddens:
+                units.append((H_GROUP, "_h", [h_sb[:, rt, :].bitcast(F32) for rt in range(ROW_TILES)]))
+            waiting = None
+            for number, (key, label, sources) in enumerate(units):
+                copy = nc.vector.tensor_copy if number == 3 else nc.scalar.copy
+                grouped = transpose_unit(number, sources, copy)
+                if waiting is not None:
+                    quantise_unit(*waiting)
+                waiting = (key, label, grouped)
+            quantise_unit(*waiting)
+
+        transpose_run(0, True)
 
         side = [per_row_tile([P, HID], F32, "side%d_" % blk) for blk in range(GATES + 1)]
+        side_banks = [5, 6, 7, 0, 1, 2, 3, 4]
         for blk in range(GATES + 1):
             for rt in range(ROW_TILES):
-                side_ps = next_bank([P, HID], F32, "side_ps")
+                side_ps = bank(side_banks[blk * ROW_TILES + rt], [P, HID], F32, "side_ps")
                 nc.tensor.matmul(
                     side_ps[:],
                     lhsT=side_lhsT[:, rt * P : (rt + 1) * P],
@@ -198,15 +198,34 @@ def tile_phiaslossengine_pb_k_kernel(
             out=blend[:], in0=ident[:], scalar=0.85, in1=blend[:], op0=ALU.mult, op1=ALU.add
         )
 
+        rz_planes.append(new_planes(CHUNK_GROUPS, 2 * HID, "rz_planes2"))
+        rz_planes.append(new_planes(CHUNK_GROUPS, 2 * HID, "rz_planes3"))
+        hh_planes = new_planes(1, GATE_COLS, "hh_planes")
+        hh_words = keep.tile([P, 2 * GATE_COLS], U8, align_bytes=64)
+        load_rz(2)
+        for rt in range(ROW_TILES):
+            load_x(3 * CHUNK_GROUPS, CHUNK_GROUPS, rt)
+        load_scale_rows(hh_planes, W_hh_scales)
+        load_rz(3)
+        nc.sync.dma_start(out=hh_words[:].bitcast(I32), in_=W_hh_words[0].bitcast(I32))
+
+        n_words = []
+        n_planes = []
+
         def mx_pass(target, kg, rt, blk, first_col, width, start, stop):
             if kg == H_GROUP:
-                lhsT, lhsT_scale = h_words[:, rt, :], h_planes[:, rt, :]
+                lhsT, lhsT_scale = a_words[H_GROUP][:, rt, :], a_planes[H_GROUP][:, rt, :]
                 rhs = hh_words[:, blk * 2 * HID : (blk + 1) * 2 * HID]
                 rhs_scale = hh_planes[:, 0, blk * HID : (blk + 1) * HID]
             else:
-                lhsT, lhsT_scale = a_words[:, rt, kg, :], a_planes[:, rt, kg, :]
-                rhs = io_words[blk][kg // WORD_CHUNK_GROUPS][:, kg % WORD_CHUNK_GROUPS, :]
-                rhs_scale = io_planes[blk][kg // SCALE_RUN_GROUPS][:, kg % SCALE_RUN_GROUPS, :]
+                unit = (kg - kg % UNIT_GROUPS, rt)
+                lhsT, lhsT_scale = a_words[unit][:, kg % UNIT_GROUPS, :], a_planes[unit][:, kg % UNIT_GROUPS, :]
+                if blk == N_GATE:
+                    rhs = n_words[kg // N_WORD_GROUPS][:, kg % N_WORD_GROUPS, :]
+                    rhs_scale = n_planes[0][:, kg, :]
+                else:
+                    rhs = rz_words[kg // RZ_WORD_GROUPS][:, kg % RZ_WORD_GROUPS, blk * 2 * HID : (blk + 1) * 2 * HID]
+                    rhs_scale = rz_planes[kg // CHUNK_GROUPS][:, kg % CHUNK_GROUPS, blk * HID : (blk + 1) * HID]
             nc.tensor.matmul_mx(
                 out=target,
                 lhsT=lhsT.bitcast(FP8X4),
@@ -217,36 +236,59 @@ def tile_phiaslossengine_pb_k_kernel(
                 stop=stop,
             )
 
+        sums = [[bank(5, [P, HID], F32, "r_sum0"), bank(6, [P, HID], F32, "r_sum1")],
+                [bank(7, [P, HID], F32, "z_sum0"), bank(4, [P, HID], F32, "z_sum1")]]
+
+        def rz_passes(passes):
+            for kg, blk, rt in passes:
+                mx_pass(sums[blk][rt][:], kg, rt, blk, 0, HID, start=(kg == 0), stop=(kg == IN_GROUPS - 1))
+
+        def chunk_passes(c):
+            return [
+                (kg, blk, rt)
+                for kg in range(c * CHUNK_GROUPS, (c + 1) * CHUNK_GROUPS)
+                for blk in (R_GATE, Z_GATE)
+                for rt in range(ROW_TILES)
+            ]
+
+        for c in range(CHUNKS - 1):
+            passes = chunk_passes(c)
+            rz_passes(passes[: len(passes) - HELD_BACK])
+            transpose_run(c + 1, False)
+            rz_passes(passes[len(passes) - HELD_BACK :])
+            if c == 0:
+                n_planes.append(new_planes(IN_GROUPS, HID, "n_planes"))
+                load_scale_rows(n_planes[0], W_io_scales[:, :, 2 * HID : 3 * HID])
+                for g in range(0, IN_GROUPS, N_WORD_GROUPS):
+                    n_words.append(load_words(g, N_WORD_GROUPS, 4 * HID, 2 * HID, "n_words%d" % g))
+
+        rz_passes([(H_GROUP, blk, rt) for blk in (R_GATE, Z_GATE) for rt in range(ROW_TILES)])
         h_n = per_row_tile([P, HID], F32, "h_n")
         for rt in range(ROW_TILES):
-            h_n_ps = next_bank([P, HID], F32, "h_n_ps")
+            h_n_ps = bank(rt, [P, HID], F32, "h_n_ps")
             mx_pass(h_n_ps[:], H_GROUP, rt, N_GATE, 0, HID, start=True, stop=True)
             nc.vector.tensor_add(out=h_n[rt][:], in0=h_n_ps[:], in1=side[GATES][rt][:])
 
-        def whole_gate(blk):
-            sums = [next_bank([P, HID], F32, "gate_sum") for rt in range(ROW_TILES)]
-            for kg in [H_GROUP] + list(range(IN_GROUPS)):
-                for rt in range(ROW_TILES):
-                    mx_pass(sums[rt][:], kg, rt, blk, 0, HID, start=(kg == H_GROUP), stop=(kg == IN_GROUPS - 1))
-            return sums
-
+        last = range((CHUNKS - 1) * CHUNK_GROUPS, IN_GROUPS)
         r = per_row_tile([P, HID], F32, "r")
         n_rest = per_row_tile([P, HID], F32, "n_rest")
-        sums = whole_gate(R_GATE)
-        for rt in range(ROW_TILES):
-            nc.vector.tensor_add(out=r[rt][:], in0=sums[rt][:], in1=side[R_GATE][rt][:])
-            nc.scalar.activation(out=r[rt][:], in_=r[rt][:], func=ACT.Sigmoid)
-        for rt in range(ROW_TILES):
-            nc.vector.tensor_mul(out=n_rest[rt][:], in0=r[rt][:], in1=h_n[rt][:])
-            nc.vector.tensor_add(out=n_rest[rt][:], in0=n_rest[rt][:], in1=side[N_GATE][rt][:])
-
         z_in = per_row_tile([P, HID], F32, "z_in")
         z = per_row_tile([P, HID], F32, "z")
         one_minus_z = per_row_tile([P, HID], F32, "one_minus_z")
         z_h = per_row_tile([P, HID], F32, "z_h")
-        sums = whole_gate(Z_GATE)
         for rt in range(ROW_TILES):
-            nc.vector.tensor_add(out=z_in[rt][:], in0=sums[rt][:], in1=side[Z_GATE][rt][:])
+            rz_passes([(kg, R_GATE, rt) for kg in last])
+            nc.vector.tensor_add(out=r[rt][:], in0=sums[R_GATE][rt][:], in1=side[R_GATE][rt][:])
+            nc.scalar.activation(out=r[rt][:], in_=r[rt][:], func=ACT.Sigmoid)
+
+        def rest_of_n(rt):
+            nc.vector.tensor_mul(out=n_rest[rt][:], in0=r[rt][:], in1=h_n[rt][:])
+            nc.vector.tensor_add(out=n_rest[rt][:], in0=n_rest[rt][:], in1=side[N_GATE][rt][:])
+
+        for rt in range(ROW_TILES):
+            rz_passes([(kg, Z_GATE, rt) for kg in last])
+            rest_of_n(rt)
+            nc.vector.tensor_add(out=z_in[rt][:], in0=sums[Z_GATE][rt][:], in1=side[Z_GATE][rt][:])
             nc.scalar.activation(out=z[rt][:], in_=z_in[rt][:], func=ACT.Sigmoid)
             nc.scalar.activation(out=one_minus_z[rt][:], in_=z_in[rt][:], func=ACT.Sigmoid, scale=-1.0)
         for rt in range(ROW_TILES):
@@ -262,13 +304,13 @@ def tile_phiaslossengine_pb_k_kernel(
             mixer.tensor_tensor(out=new_h[rt][:, cols], in0=one_minus_z[rt][:, cols], in1=n[rt][:, cols], op=ALU.mult)
             mixer.tensor_tensor(out=new_h[rt][:, cols], in0=new_h[rt][:, cols], in1=z_h[rt][:, cols], op=ALU.add)
 
-        def smooth_and_store(rt, cols, width):
-            out_ps = next_bank([P, width], F32, "out_ps")
+        def smooth_and_store(number, rt, cols, width):
+            out_ps = bank(number, [P, width], F32, "out_ps")
             nc.tensor.matmul(out_ps[:], lhsT=blend[:], rhs=new_h[rt][:, cols], start=True, stop=True)
             nc.scalar.copy(out=out_sb[rt][:, cols], in_=out_ps[:])
             nc.sync.dma_start(out=out[rt * P : (rt + 1) * P, cols], in_=out_sb[rt][:, cols])
 
-        i_n = next_bank([P, HID], F32, "i_n")
+        i_n = bank(2, [P, HID], F32, "i_n")
         for g in range(IN_GROUPS):
             mx_pass(i_n[:], g, 0, N_GATE, 0, HID, start=(g == 0), stop=(g == IN_GROUPS - 1))
         halves = [slice(0, HALF), slice(HALF, HID)]
@@ -276,13 +318,15 @@ def tile_phiaslossengine_pb_k_kernel(
             mix(0, cols, i_n[:, cols], nc.gpsimd)
 
         quarters = [slice(q * QUARTER, (q + 1) * QUARTER) for q in range(HID // QUARTER)]
+        quarter_banks = [3, 0, 1, 5]
+        out_banks = [6, 7, 4]
         for q, cols in enumerate(quarters):
-            i_n = next_bank([P, QUARTER], F32, "i_n_quarter")
+            i_n = bank(quarter_banks[q], [P, QUARTER], F32, "i_n_quarter")
             for g in range(IN_GROUPS):
                 mx_pass(i_n[:], g, 1, N_GATE, q * QUARTER, QUARTER, start=(g == 0), stop=(g == IN_GROUPS - 1))
             mix(1, cols, i_n[:], nc.vector)
             if q > 0:
-                smooth_and_store(1, quarters[q - 1], QUARTER)
-        for cols in halves:
-            smooth_and_store(0, cols, HALF)
-        smooth_and_store(1, quarters[-1], QUARTER)
+                smooth_and_store(out_banks[q - 1], 1, quarters[q - 1], QUARTER)
+        smooth_and_store(2, 0, halves[0], HALF)
+        smooth_and_store(3, 0, halves[1], HALF)
+        smooth_and_store(0, 1, quarters[-1], QUARTER)

@@ -64,13 +64,8 @@ def tile_phiaslossengine_pb_k_kernel(
         blend = keep.tile([P, P], F32)
         nc.vector.memset(side_lhsT[:], 1.0)
         nc.vector.memset(side_rhs[:], 0.0)
-        nc.vector.memset(table_warmer[:], 0.0)
+        nc.gpsimd.memset(table_warmer[:], 0.0)
         make_identity(nc, ident[:])
-        nc.scalar.dma_start(out=side_lhsT[0:1, :], in_=tension.rearrange("n o -> o n"))
-        nc.scalar.dma_start(out=side_rhs[0:1, 0:GATE_COLS], in_=w_it.unsqueeze(0))
-        nc.scalar.dma_start(out=side_rhs[1:2, 0:GATE_COLS], in_=b_ih.unsqueeze(0))
-        nc.scalar.dma_start(out=side_rhs[2:3, 0 : 2 * HID], in_=b_hh[0 : 2 * HID].unsqueeze(0))
-        nc.scalar.dma_start(out=side_rhs[2:3, GATE_COLS:], in_=b_hh[2 * HID :].unsqueeze(0))
         nc.scalar.activation(out=table_warmer[:], in_=table_warmer[:], func=ACT.Sigmoid)
         nc.gpsimd.memset(blend[:], 0.0)
         for f in range(P // FACTION):
@@ -95,11 +90,10 @@ def tile_phiaslossengine_pb_k_kernel(
             return planes
 
         def load_scale_rows(planes, rows):
-            for q in range(SCALE_ROWS // 2):
-                first = 32 * (q // 4) + q % 4
+            for q in range(SCALE_ROWS // 4):
                 nc.sync.dma_start(
-                    out=planes[first:P:64].bitcast(I32),
-                    in_=rows[:, q : SCALE_ROWS : SCALE_ROWS // 2, :].rearrange("g q n -> q g n").bitcast(I32),
+                    out=planes[q:P:32].bitcast(I32),
+                    in_=rows[:, q : SCALE_ROWS : SCALE_ROWS // 4, :].rearrange("g q n -> q g n").bitcast(I32),
                 )
 
         def load_words(first_group, groups, first_byte, n_bytes, name):
@@ -125,9 +119,13 @@ def tile_phiaslossengine_pb_k_kernel(
         h_sb = keep.tile([P, ROW_TILES, HID], BF16)
         rz_planes.append(new_planes(CHUNK_GROUPS, 2 * HID, "rz_planes0"))
         rz_planes.append(new_planes(CHUNK_GROUPS, 2 * HID, "rz_planes1"))
-        for g in range(0, CHUNK_GROUPS, UNIT_GROUPS):
-            for rt in range(ROW_TILES):
-                load_x(g, UNIT_GROUPS, rt)
+        for rt in range(ROW_TILES):
+            load_x(0, CHUNK_GROUPS, rt)
+        nc.sync.dma_start(out=side_lhsT[0:1, :], in_=tension.rearrange("n o -> o n"))
+        nc.sync.dma_start(out=side_rhs[0:1, 0:GATE_COLS], in_=w_it.unsqueeze(0))
+        nc.sync.dma_start(out=side_rhs[1:2, 0:GATE_COLS], in_=b_ih.unsqueeze(0))
+        nc.sync.dma_start(out=side_rhs[2:3, 0 : 2 * HID], in_=b_hh[0 : 2 * HID].unsqueeze(0))
+        nc.sync.dma_start(out=side_rhs[2:3, GATE_COLS:], in_=b_hh[2 * HID :].unsqueeze(0))
         nc.sync.dma_start(out=h_sb[:], in_=hiddens.rearrange("(r p) k -> p r k", p=P))
         load_rz(0)
         for rt in range(ROW_TILES):
@@ -162,8 +160,8 @@ def tile_phiaslossengine_pb_k_kernel(
 
         def transpose_run(c, with_hiddens):
             units = []
-            for g in range(c * CHUNK_GROUPS, (c + 1) * CHUNK_GROUPS, UNIT_GROUPS):
-                for rt in range(ROW_TILES):
+            for rt in range(ROW_TILES):
+                for g in range(c * CHUNK_GROUPS, (c + 1) * CHUNK_GROUPS, UNIT_GROUPS):
                     pairs = x_pairs[(g, rt)]
                     units.append(((g, rt), "%d_%d" % (g, rt), [pairs[:, 0:PAIRS], pairs[:, PAIRS : 2 * PAIRS]]))
             if with_hiddens:

@@ -74,9 +74,9 @@ def tile_phiaslossengine_pb_k_kernel(
 
         x_pairs = {}
 
-        def load_x(first_group, groups, rt):
+        def load_x(queue, first_group, groups, rt):
             x_sb = keep.tile([P, groups * K_PASS], BF16, name="x_sb%d_%d" % (first_group, rt))
-            nc.sync.dma_start(
+            queue.dma_start(
                 out=x_sb[:],
                 in_=ag_diff[rt * P : (rt + 1) * P, first_group * K_PASS : (first_group + groups) * K_PASS],
             )
@@ -120,7 +120,7 @@ def tile_phiaslossengine_pb_k_kernel(
         rz_planes.append(new_planes(CHUNK_GROUPS, 2 * HID, "rz_planes0"))
         rz_planes.append(new_planes(CHUNK_GROUPS, 2 * HID, "rz_planes1"))
         for rt in range(ROW_TILES):
-            load_x(0, CHUNK_GROUPS, rt)
+            load_x(nc.sync, 0, CHUNK_GROUPS, rt)
         nc.sync.dma_start(out=side_lhsT[0:1, :], in_=tension.rearrange("n o -> o n"))
         nc.sync.dma_start(out=side_rhs[0:1, 0:GATE_COLS], in_=w_it.unsqueeze(0))
         nc.sync.dma_start(out=side_rhs[1:2, 0:GATE_COLS], in_=b_ih.unsqueeze(0))
@@ -128,11 +128,10 @@ def tile_phiaslossengine_pb_k_kernel(
         nc.sync.dma_start(out=side_rhs[2:3, GATE_COLS:], in_=b_hh[2 * HID :].unsqueeze(0))
         nc.sync.dma_start(out=h_sb[:], in_=hiddens.rearrange("(r p) k -> p r k", p=P))
         load_rz(0)
-        for rt in range(ROW_TILES):
-            load_x(CHUNK_GROUPS, CHUNK_GROUPS, rt)
         load_rz(1)
-        for rt in range(ROW_TILES):
-            load_x(2 * CHUNK_GROUPS, CHUNK_GROUPS, rt)
+        for c in range(1, CHUNKS):
+            for rt in range(ROW_TILES):
+                load_x(nc.gpsimd, c * CHUNK_GROUPS, CHUNK_GROUPS, rt)
 
         a_words = {}
         a_planes = {}
@@ -201,8 +200,6 @@ def tile_phiaslossengine_pb_k_kernel(
         hh_planes = new_planes(1, GATE_COLS, "hh_planes")
         hh_words = keep.tile([P, 2 * GATE_COLS], U8, align_bytes=64)
         load_rz(2)
-        for rt in range(ROW_TILES):
-            load_x(3 * CHUNK_GROUPS, CHUNK_GROUPS, rt)
         load_scale_rows(hh_planes, W_hh_scales)
         load_rz(3)
         nc.sync.dma_start(out=hh_words[:].bitcast(I32), in_=W_hh_words[0].bitcast(I32))

@@ -136,11 +136,19 @@ def tile_phiaslossengine_pb_k_kernel(
         a_words = {}
         a_planes = {}
 
-        def transpose_unit(number, sources, copy):
+        def split_unit(pairs):
+            split_words = stage.tile([P, 2, 2, P], F32)
+            nc.vector.tensor_copy(out=split_words[:], in_=pairs.rearrange("p (s c u) -> p s u c", s=2, u=2))
+            return split_words[:]
+
+        def as_it_lies(pairs):
+            return pairs.rearrange("p (s c u) -> p s u c", s=2, u=2)
+
+        def transpose_unit(number, split_words, copy):
             flipped = bank(number, [P, 2, 2, P], F32, "flipped")
             for s in range(2):
                 for u in range(2):
-                    nc.tensor.transpose(flipped[:, s, u, :], sources[s][:, u:PAIRS:2], ident[:])
+                    nc.tensor.transpose(flipped[:, s, u, :], split_words[:, s, u, :], ident[:])
             grouped = stage.tile([P, 2 * P * 4], BF16, align_bytes=64)
             copy(
                 out=grouped[:].bitcast(F32).rearrange("p (s c u) -> p s c u", s=2, u=2),
@@ -157,24 +165,33 @@ def tile_phiaslossengine_pb_k_kernel(
                 in_=grouped[:],
             )
 
-        def transpose_run(c, with_hiddens):
-            units = []
-            for rt in range(ROW_TILES):
-                for g in range(c * CHUNK_GROUPS, (c + 1) * CHUNK_GROUPS, UNIT_GROUPS):
-                    pairs = x_pairs[(g, rt)]
-                    units.append(((g, rt), "%d_%d" % (g, rt), [pairs[:, 0:PAIRS], pairs[:, PAIRS : 2 * PAIRS]]))
-            if with_hiddens:
-                units.append((H_GROUP, "_h", [h_sb[:, rt, :].bitcast(F32) for rt in range(ROW_TILES)]))
+        def split_chunk(c):
+            if c == 0:
+                keys = [(g, rt) for rt in range(ROW_TILES) for g in range(0, CHUNK_GROUPS, UNIT_GROUPS)]
+            else:
+                keys = [
+                    (g, rt)
+                    for g in range(c * CHUNK_GROUPS, (c + 1) * CHUNK_GROUPS, UNIT_GROUPS)
+                    for rt in range(ROW_TILES)
+                ]
+            if c == 0:
+                units = [(key, "%d_%d" % key, as_it_lies(x_pairs[key])) for key in keys]
+                units.append((H_GROUP, "_h", as_it_lies(h_sb[:].rearrange("p r k -> p (r k)").bitcast(F32))))
+            else:
+                units = [(key, "%d_%d" % key, split_unit(x_pairs[key])) for key in keys]
+            return units
+
+        def transpose_run(units, vector_empties):
             waiting = None
-            for number, (key, label, sources) in enumerate(units):
-                copy = nc.vector.tensor_copy if number == 3 else nc.scalar.copy
-                grouped = transpose_unit(number, sources, copy)
+            for number, (key, label, split_words) in enumerate(units):
+                copy = nc.vector.tensor_copy if number in vector_empties else nc.scalar.copy
+                grouped = transpose_unit(number, split_words, copy)
                 if waiting is not None:
                     quantise_unit(*waiting)
                 waiting = (key, label, grouped)
             quantise_unit(*waiting)
 
-        transpose_run(0, True)
+        transpose_run(split_chunk(0), [3])
 
         side = [per_row_tile([P, HID], F32, "side%d_" % blk) for blk in range(GATES + 1)]
         side_banks = [5, 6, 7, 0, 1, 2, 3, 4]
@@ -248,8 +265,9 @@ def tile_phiaslossengine_pb_k_kernel(
 
         for c in range(CHUNKS - 1):
             passes = chunk_passes(c)
+            units = split_chunk(c + 1)
             rz_passes(passes[: len(passes) - HELD_BACK])
-            transpose_run(c + 1, False)
+            transpose_run(units, [])
             rz_passes(passes[len(passes) - HELD_BACK :])
             if c == 0:
                 n_planes.append(new_planes(IN_GROUPS, HID, "n_planes"))

@@ -218,8 +218,8 @@ def tile_phiaslossengine_pb_k_kernel(
         hh_words = keep.tile([P, 2 * GATE_COLS], U8, align_bytes=64)
         load_rz(2)
         load_scale_rows(hh_planes, W_hh_scales)
-        load_rz(3)
         nc.sync.dma_start(out=hh_words[:].bitcast(I32), in_=W_hh_words[0].bitcast(I32))
+        load_rz(3)
 
         n_words = []
         n_planes = []
@@ -338,8 +338,9 @@ def tile_phiaslossengine_pb_k_kernel(
             for g in range(IN_GROUPS):
                 mx_pass(i_n[:], g, 1, N_GATE, q * QUARTER, QUARTER, start=(g == 0), stop=(g == IN_GROUPS - 1))
             mix(1, cols, i_n[:], nc.vector)
-            if q > 0:
-                smooth_and_store(out_banks[q - 1], 1, quarters[q - 1], QUARTER)
+            if q > 1:
+                smooth_and_store(out_banks[q - 2], 1, quarters[q - 2], QUARTER)
+        smooth_and_store(out_banks[2], 1, quarters[2], QUARTER)
         smooth_and_store(2, 0, halves[0], HALF)
         smooth_and_store(3, 0, halves[1], HALF)
-        smooth_and_store(0, 1, quarters[-1], QUARTER)
+        smooth_and_store(0, 1, quarters[3], QUARTER)

@@ -34,6 +34,7 @@ CHUNK_GROUPS = 4
 CHUNKS = IN_GROUPS // CHUNK_GROUPS
 RZ_WORD_GROUPS = 2
 N_WORD_GROUPS = 4
+WARM_UP_MATMULS = 5
 HELD_BACK = 4
 HALF = HID // 2
 QUARTER = HID // 4
@@ -62,6 +63,11 @@ def tile_phiaslossengine_pb_k_kernel(
         table_warmer = keep.tile([P, 1], F32)
         ident = keep.tile([P, P], F32)
         blend = keep.tile([P, P], F32)
+        warm = keep.tile([P, HID], BF16)
+        nc.vector.memset(warm[:], 0.0)
+        warm_ps = bank(7, [P, HID], F32, "warm_ps")
+        for i in range(WARM_UP_MATMULS):
+            nc.tensor.matmul(warm_ps[:], lhsT=warm[:, 0:P], rhs=warm[:], start=True, stop=True)
         nc.vector.memset(side_lhsT[:], 1.0)
         nc.vector.memset(side_rhs[:], 0.0)
         nc.gpsimd.memset(table_warmer[:], 0.0)
@@ -193,10 +199,12 @@ def tile_phiaslossengine_pb_k_kernel(
 
         transpose_run(split_chunk(0), [3])
 
-        side = [per_row_tile([P, HID], F32, "side%d_" % blk) for blk in range(GATES + 1)]
-        side_banks = [5, 6, 7, 0, 1, 2, 3, 4]
+        side = [per_row_tile([P, HID], F32, "side%d_" % blk) for blk in range(GATES)]
+        side_h_n = keep.tile([P, HID], F32)
+        side.append([side_h_n, side_h_n])
+        side_banks = [5, 6, 7, 0, 1, 2, 3]
         for blk in range(GATES + 1):
-            for rt in range(ROW_TILES):
+            for rt in range(ROW_TILES if blk < GATES else 1):
                 side_ps = bank(side_banks[blk * ROW_TILES + rt], [P, HID], F32, "side_ps")
                 nc.tensor.matmul(
                     side_ps[:],
@@ -311,11 +319,15 @@ def tile_phiaslossengine_pb_k_kernel(
         new_h = per_row_tile([P, HID], F32, "new_h")
         out_sb = per_row_tile([P, HID], F32, "out_sb")
 
-        def mix(rt, cols, i_n, mixer):
+        def make_n(rt, cols, i_n):
             nc.vector.tensor_add(out=n[rt][:, cols], in0=i_n, in1=n_rest[rt][:, cols])
             nc.scalar.activation(out=n[rt][:, cols], in_=n[rt][:, cols], func=ACT.Tanh)
-            mixer.tensor_tensor(out=new_h[rt][:, cols], in0=one_minus_z[rt][:, cols], in1=n[rt][:, cols], op=ALU.mult)
-            mixer.tensor_tensor(out=new_h[rt][:, cols], in0=new_h[rt][:, cols], in1=z_h[rt][:, cols], op=ALU.add)
+
+        def mix_multiply(rt, cols):
+            nc.vector.tensor_mul(out=new_h[rt][:, cols], in0=one_minus_z[rt][:, cols], in1=n[rt][:, cols])
+
+        def mix_add(rt, cols):
+            nc.vector.tensor_add(out=new_h[rt][:, cols], in0=new_h[rt][:, cols], in1=z_h[rt][:, cols])
 
         def smooth_and_store(number, rt, cols, width):
             out_ps = bank(number, [P, width], F32, "out_ps")
@@ -328,7 +340,8 @@ def tile_phiaslossengine_pb_k_kernel(
             mx_pass(i_n[:], g, 0, N_GATE, 0, HID, start=(g == 0), stop=(g == IN_GROUPS - 1))
         halves = [slice(0, HALF), slice(HALF, HID)]
         for cols in halves:
-            mix(0, cols, i_n[:, cols], nc.gpsimd)
+            make_n(0, cols, i_n[:, cols])
+        fillers = [(mix_multiply, halves[0]), (mix_add, halves[0]), (mix_multiply, halves[1]), (mix_add, halves[1])]
 
         quarters = [slice(q * QUARTER, (q + 1) * QUARTER) for q in range(HID // QUARTER)]
         quarter_banks = [3, 0, 1, 5]
@@ -337,7 +350,11 @@ def tile_phiaslossengine_pb_k_kernel(
             i_n = bank(quarter_banks[q], [P, QUARTER], F32, "i_n_quarter")
             for g in range(IN_GROUPS):
                 mx_pass(i_n[:], g, 1, N_GATE, q * QUARTER, QUARTER, start=(g == 0), stop=(g == IN_GROUPS - 1))
-            mix(1, cols, i_n[:], nc.vector)
+            make_n(1, cols, i_n[:])
+            step, filler_cols = fillers[q]
+            step(0, filler_cols)
+            mix_multiply(1, cols)
+            mix_add(1, cols)
             if q > 1:
                 smooth_and_store(out_banks[q - 2], 1, quarters[q - 2], QUARTER)
         smooth_and_store(out_banks[2], 1, quarters[2], QUARTER)

@@ -116,10 +116,11 @@ def tile_phiaslossengine_pb_k_kernel(
         rz_words = []
 
         def load_rz(c):
-            load_scale_rows(
-                rz_planes[c], W_io_scales[c * CHUNK_GROUPS : (c + 1) * CHUNK_GROUPS, :, 0 : 2 * HID]
-            )
-            for g in range(c * CHUNK_GROUPS, (c + 1) * CHUNK_GROUPS, RZ_WORD_GROUPS):
+            first = c * CHUNK_GROUPS
+            if c == 0:
+                rz_words.append(load_words(first, RZ_WORD_GROUPS, 0, 4 * HID, "rz_words%d" % first))
+            load_scale_rows(rz_planes[c], W_io_scales[first : first + CHUNK_GROUPS, :, 0 : 2 * HID])
+            for g in range(first + (RZ_WORD_GROUPS if c == 0 else 0), first + CHUNK_GROUPS, RZ_WORD_GROUPS):
                 rz_words.append(load_words(g, RZ_WORD_GROUPS, 0, 4 * HID, "rz_words%d" % g))
 
         h_sb = keep.tile([P, ROW_TILES, HID], BF16)

from contextlib import ExitStack

import concourse.mybir as mybir
from concourse.masks import make_identity

F32 = mybir.dt.float32
BF16 = mybir.dt.bfloat16
I32 = mybir.dt.int32
U32 = mybir.dt.uint32
U8 = mybir.dt.uint8
FP8X4 = mybir.dt.float8_e4m3fn_x4
FP4X4 = mybir.dt.float4_e2m1fn_x4
ALU = mybir.AluOpType
ACT = mybir.ActivationFunctionType

P = 128
K_PASS = 512
PAIRS = K_PASS // 2
CELLS = 256
ROW_TILES = CELLS // P
K_IN = 8192
HID = 512
FACTION = 32
GATES = 3
R_GATE, Z_GATE, N_GATE = 0, 1, 2
GATE_COLS = GATES * HID
IN_GROUPS = K_IN // K_PASS
H_GROUP = IN_GROUPS
PSUM_BANKS = 8
SCALE_ROWS = 16

UNIT_GROUPS = 2
CHUNK_GROUPS = 4
CHUNKS = IN_GROUPS // CHUNK_GROUPS
RZ_WORD_GROUPS = 2
N_WORD_GROUPS = 4
WARM_UP_MATMULS = 5
HELD_BACK = 4
HALF = HID // 2
QUARTER = HID // 4

FLOPS = 2 * CELLS * (K_IN + HID) * GATE_COLS


def tile_phiaslossengine_pb_k_kernel(
    tc, ag_diff, tension, hiddens, W_io_words, W_io_scales, w_it, W_hh_words, W_hh_scales, b_ih, b_hh, out
):
    nc = tc.nc
    with ExitStack() as stack:
        stack.enter_context(tc.manual_schedule())
        keep = stack.enter_context(tc.tile_pool(name="keep", bufs=1))
        stage = stack.enter_context(tc.tile_pool(name="stage", bufs=5))
        psum = stack.enter_context(tc.psum_pool(name="psum", bufs=1))

        def bank(number, shape, dtype, name):
            return psum.tile(shape, dtype, tag="bank%d" % number, name=name)

        def per_row_tile(shape, dtype, name):
            return [keep.tile(shape, dtype, name="%s%d" % (name, rt)) for rt in range(ROW_TILES)]

        side_lhsT = keep.tile([P, CELLS], BF16)
        side_rhs = keep.tile([P, (GATES + 1) * HID], BF16)
        table_warmer = keep.tile([P, 1], F32)
        ident = keep.tile([P, P], F32)
        blend = keep.tile([P, P], F32)
        warm = keep.tile([P, HID], BF16)
        nc.vector.memset(warm[:], 0.0)
        warm_ps = bank(7, [P, HID], F32, "warm_ps")
        for i in range(WARM_UP_MATMULS):
            nc.tensor.matmul(warm_ps[:], lhsT=warm[:, 0:P], rhs=warm[:], start=True, stop=True)
        nc.vector.memset(side_lhsT[:], 1.0)
        nc.vector.memset(side_rhs[:], 0.0)
        nc.gpsimd.memset(table_warmer[:], 0.0)
        make_identity(nc, ident[:])
        nc.scalar.activation(out=table_warmer[:], in_=table_warmer[:], func=ACT.Sigmoid)
        nc.gpsimd.memset(blend[:], 0.0)
        for f in range(P // FACTION):
            cells = slice(f * FACTION, (f + 1) * FACTION)
            nc.gpsimd.memset(blend[cells, cells], 1.0)

        x_pairs = {}

        def load_x(queue, first_group, groups, rt):
            x_sb = keep.tile([P, groups * K_PASS], BF16, name="x_sb%d_%d" % (first_group, rt))
            queue.dma_start(
                out=x_sb[:],
                in_=ag_diff[rt * P : (rt + 1) * P, first_group * K_PASS : (first_group + groups) * K_PASS],
            )
            pairs = x_sb[:].bitcast(F32)
            for place in range(0, groups, UNIT_GROUPS):
                x_pairs[(first_group + place, rt)] = pairs[:, place * PAIRS : (place + UNIT_GROUPS) * PAIRS]

        def new_planes(groups, columns, name):
            planes = keep.tile([P, groups, columns], U8, align_bytes=64, name=name)
            nc.vector.memset(planes[:].bitcast(I32), 0)
            return planes

        def load_scale_rows(planes, rows):
            for q in range(SCALE_ROWS // 4):
                nc.sync.dma_start(
                    out=planes[q:P:32].bitcast(I32),
                    in_=rows[:, q : SCALE_ROWS : SCALE_ROWS // 4, :].rearrange("g q n -> q g n").bitcast(I32),
                )

        def load_words(first_group, groups, first_byte, n_bytes, name):
            words = keep.tile([P, groups, n_bytes], U8, align_bytes=64, name=name)
            nc.sync.dma_start(
                out=words[:].bitcast(I32),
                in_=W_io_words[first_group : first_group + groups, :, first_byte : first_byte + n_bytes]
                .rearrange("g p n -> p g n")
                .bitcast(I32),
            )
            return words

        rz_planes = []
        rz_words = []

        def load_rz(c):
            first = c * CHUNK_GROUPS
            if c == 0:
                rz_words.append(load_words(first, RZ_WORD_GROUPS, 0, 4 * HID, "rz_words%d" % first))
            load_scale_rows(rz_planes[c], W_io_scales[first : first + CHUNK_GROUPS, :, 0 : 2 * HID])
            for g in range(first + (RZ_WORD_GROUPS if c == 0 else 0), first + CHUNK_GROUPS, RZ_WORD_GROUPS):
                rz_words.append(load_words(g, RZ_WORD_GROUPS, 0, 4 * HID, "rz_words%d" % g))

        h_sb = keep.tile([P, ROW_TILES, HID], BF16)
        rz_planes.append(new_planes(CHUNK_GROUPS, 2 * HID, "rz_planes0"))
        rz_planes.append(new_planes(CHUNK_GROUPS, 2 * HID, "rz_planes1"))
        for rt in range(ROW_TILES):
            load_x(nc.sync, 0, CHUNK_GROUPS, rt)
        nc.sync.dma_start(out=side_lhsT[0:1, :], in_=tension.rearrange("n o -> o n"))
        nc.sync.dma_start(out=side_rhs[0:1, 0:GATE_COLS], in_=w_it.unsqueeze(0))
        nc.sync.dma_start(out=side_rhs[1:2, 0:GATE_COLS], in_=b_ih.unsqueeze(0))
        nc.sync.dma_start(out=side_rhs[2:3, 0 : 2 * HID], in_=b_hh[0 : 2 * HID].unsqueeze(0))
        nc.sync.dma_start(out=side_rhs[2:3, GATE_COLS:], in_=b_hh[2 * HID :].unsqueeze(0))
        nc.sync.dma_start(out=h_sb[:], in_=hiddens.rearrange("(r p) k -> p r k", p=P))
        load_rz(0)
        load_rz(1)
        for c in range(1, CHUNKS):
            for rt in range(ROW_TILES):
                load_x(nc.gpsimd, c * CHUNK_GROUPS, CHUNK_GROUPS, rt)

        a_words = {}
        a_planes = {}

        def split_unit(pairs):
            split_words = stage.tile([P, 2, 2, P], F32)
            nc.vector.tensor_copy(out=split_words[:], in_=pairs.rearrange("p (s c u) -> p s u c", s=2, u=2))
            return split_words[:]

        def as_it_lies(pairs):
            return pairs.rearrange("p (s c u) -> p s u c", s=2, u=2)

        def transpose_unit(number, split_words, copy):
            flipped = bank(number, [P, 2, 2, P], F32, "flipped")
            for s in range(2):
                for u in range(2):
                    nc.tensor.transpose(flipped[:, s, u, :], split_words[:, s, u, :], ident[:])
            grouped = stage.tile([P, 2 * P * 4], BF16, align_bytes=64)
            copy(
                out=grouped[:].bitcast(F32).rearrange("p (s c u) -> p s c u", s=2, u=2),
                in_=flipped[:].rearrange("p s u c -> p s c u"),
            )
            return grouped

        def quantise_unit(key, label, grouped):
            a_words[key] = keep.tile([P, 2, P], U32, align_bytes=64, name="a_words" + label)
            a_planes[key] = keep.tile([P, 2, P], U8, align_bytes=64, name="a_planes" + label)
            nc.vector.quantize_mx(
                out=a_words[key][:].rearrange("p s c -> p (s c)").bitcast(FP8X4),
                scales=a_planes[key][:].rearrange("p s c -> p (s c)"),
                in_=grouped[:],
            )

        def split_chunk(c):
            if c == 0:
                keys = [(g, rt) for rt in range(ROW_TILES) for g in range(0, CHUNK_GROUPS, UNIT_GROUPS)]
            else:
                keys = [
                    (g, rt)
                    for g in range(c * CHUNK_GROUPS, (c + 1) * CHUNK_GROUPS, UNIT_GROUPS)
                    for rt in range(ROW_TILES)
                ]
            if c == 0:
                units = [(key, "%d_%d" % key, as_it_lies(x_pairs[key])) for key in keys]
                units.append((H_GROUP, "_h", as_it_lies(h_sb[:].rearrange("p r k -> p (r k)").bitcast(F32))))
            else:
                units = [(key, "%d_%d" % key, split_unit(x_pairs[key])) for key in keys]
            return units

        def transpose_run(units, vector_empties):
            waiting = None
            for number, (key, label, split_words) in enumerate(units):
                copy = nc.vector.tensor_copy if number in vector_empties else nc.scalar.copy
                grouped = transpose_unit(number, split_words, copy)
                if waiting is not None:
                    quantise_unit(*waiting)
                waiting = (key, label, grouped)
            quantise_unit(*waiting)

        transpose_run(split_chunk(0), [3])

        side = [per_row_tile([P, HID], F32, "side%d_" % blk) for blk in range(GATES)]
        side_h_n = keep.tile([P, HID], F32)
        side.append([side_h_n, side_h_n])
        side_banks = [5, 6, 7, 0, 1, 2, 3]
        for blk in range(GATES + 1):
            for rt in range(ROW_TILES if blk < GATES else 1):
                side_ps = bank(side_banks[blk * ROW_TILES + rt], [P, HID], F32, "side_ps")
                nc.tensor.matmul(
                    side_ps[:],
                    lhsT=side_lhsT[:, rt * P : (rt + 1) * P],
                    rhs=side_rhs[:, blk * HID : (blk + 1) * HID],
                    start=True,
                    stop=True,
                )
                copy = nc.scalar.copy if rt == 0 else nc.vector.tensor_copy
                copy(out=side[blk][rt][:], in_=side_ps[:])
        nc.vector.tensor_scalar_mul(out=blend[:], in0=blend[:], scalar1=0.15 / FACTION)
        nc.vector.scalar_tensor_tensor(
            out=blend[:], in0=ident[:], scalar=0.85, in1=blend[:], op0=ALU.mult, op1=ALU.add
        )

        rz_planes.append(new_planes(CHUNK_GROUPS, 2 * HID, "rz_planes2"))
        rz_planes.append(new_planes(CHUNK_GROUPS, 2 * HID, "rz_planes3"))
        hh_planes = new_planes(1, GATE_COLS, "hh_planes")
        hh_words = keep.tile([P, 2 * GATE_COLS], U8, align_bytes=64)
        load_rz(2)
        load_scale_rows(hh_planes, W_hh_scales)
        nc.sync.dma_start(out=hh_words[:].bitcast(I32), in_=W_hh_words[0].bitcast(I32))
        load_rz(3)

        n_words = []
        n_planes = []

        def mx_pass(target, kg, rt, blk, first_col, width, start, stop):
            if kg == H_GROUP:
                lhsT, lhsT_scale = a_words[H_GROUP][:, rt, :], a_planes[H_GROUP][:, rt, :]
                rhs = hh_words[:, blk * 2 * HID : (blk + 1) * 2 * HID]
                rhs_scale = hh_planes[:, 0, blk * HID : (blk + 1) * HID]
            else:
                unit = (kg - kg % UNIT_GROUPS, rt)
                lhsT, lhsT_scale = a_words[unit][:, kg % UNIT_GROUPS, :], a_planes[unit][:, kg % UNIT_GROUPS, :]
                if blk == N_GATE:
                    rhs = n_words[kg // N_WORD_GROUPS][:, kg % N_WORD_GROUPS, :]
                    rhs_scale = n_planes[0][:, kg, :]
                else:
                    rhs = rz_words[kg // RZ_WORD_GROUPS][:, kg % RZ_WORD_GROUPS, blk * 2 * HID : (blk + 1) * 2 * HID]
                    rhs_scale = rz_planes[kg // CHUNK_GROUPS][:, kg % CHUNK_GROUPS, blk * HID : (blk + 1) * HID]
            nc.tensor.matmul_mx(
                out=target,
                lhsT=lhsT.bitcast(FP8X4),
                lhsT_scale=lhsT_scale,
                rhs=rhs[:, 2 * first_col : 2 * (first_col + width)].bitcast(FP4X4),
                rhs_scale=rhs_scale[:, first_col : first_col + width],
                start=start,
                stop=stop,
            )

        sums = [[bank(5, [P, HID], F32, "r_sum0"), bank(6, [P, HID], F32, "r_sum1")],
                [bank(7, [P, HID], F32, "z_sum0"), bank(4, [P, HID], F32, "z_sum1")]]

        def rz_passes(passes):
            for kg, blk, rt in passes:
                mx_pass(sums[blk][rt][:], kg, rt, blk, 0, HID, start=(kg == 0), stop=(kg == IN_GROUPS - 1))

        def chunk_passes(c):
            return [
                (kg, blk, rt)
                for kg in range(c * CHUNK_GROUPS, (c + 1) * CHUNK_GROUPS)
                for blk in (R_GATE, Z_GATE)
                for rt in range(ROW_TILES)
            ]

        for c in range(CHUNKS - 1):
            passes = chunk_passes(c)
            units = split_chunk(c + 1)
            rz_passes(passes[: len(passes) - HELD_BACK])
            transpose_run(units, [])
            rz_passes(passes[len(passes) - HELD_BACK :])
            if c == 0:
                n_planes.append(new_planes(IN_GROUPS, HID, "n_planes"))
                load_scale_rows(n_planes[0], W_io_scales[:, :, 2 * HID : 3 * HID])
                for g in range(0, IN_GROUPS, N_WORD_GROUPS):
                    n_words.append(load_words(g, N_WORD_GROUPS, 4 * HID, 2 * HID, "n_words%d" % g))

        rz_passes([(H_GROUP, blk, rt) for blk in (R_GATE, Z_GATE) for rt in range(ROW_TILES)])
        h_n = per_row_tile([P, HID], F32, "h_n")
        for rt in range(ROW_TILES):
            h_n_ps = bank(rt, [P, HID], F32, "h_n_ps")
            mx_pass(h_n_ps[:], H_GROUP, rt, N_GATE, 0, HID, start=True, stop=True)
            nc.vector.tensor_add(out=h_n[rt][:], in0=h_n_ps[:], in1=side[GATES][rt][:])

        last = range((CHUNKS - 1) * CHUNK_GROUPS, IN_GROUPS)
        r = per_row_tile([P, HID], F32, "r")
        n_rest = per_row_tile([P, HID], F32, "n_rest")
        z_in = per_row_tile([P, HID], F32, "z_in")
        z = per_row_tile([P, HID], F32, "z")
        one_minus_z = per_row_tile([P, HID], F32, "one_minus_z")
        z_h = per_row_tile([P, HID], F32, "z_h")
        for rt in range(ROW_TILES):
            rz_passes([(kg, R_GATE, rt) for kg in last])
            nc.vector.tensor_add(out=r[rt][:], in0=sums[R_GATE][rt][:], in1=side[R_GATE][rt][:])
            nc.scalar.activation(out=r[rt][:], in_=r[rt][:], func=ACT.Sigmoid)

        def rest_of_n(rt):
            nc.vector.tensor_mul(out=n_rest[rt][:], in0=r[rt][:], in1=h_n[rt][:])
            nc.vector.tensor_add(out=n_rest[rt][:], in0=n_rest[rt][:], in1=side[N_GATE][rt][:])

        for rt in range(ROW_TILES):
            rz_passes([(kg, Z_GATE, rt) for kg in last])
            rest_of_n(rt)
            nc.vector.tensor_add(out=z_in[rt][:], in0=sums[Z_GATE][rt][:], in1=side[Z_GATE][rt][:])
            nc.scalar.activation(out=z[rt][:], in_=z_in[rt][:], func=ACT.Sigmoid)
            nc.scalar.activation(out=one_minus_z[rt][:], in_=z_in[rt][:], func=ACT.Sigmoid, scale=-1.0)
        for rt in range(ROW_TILES):
            nc.vector.tensor_mul(out=z_h[rt][:], in0=z[rt][:], in1=h_sb[:, rt, :])

        n = per_row_tile([P, HID], F32, "n")
        new_h = per_row_tile([P, HID], F32, "new_h")
        out_sb = per_row_tile([P, HID], F32, "out_sb")

        def make_n(rt, cols, i_n):
            nc.vector.tensor_add(out=n[rt][:, cols], in0=i_n, in1=n_rest[rt][:, cols])
            nc.scalar.activation(out=n[rt][:, cols], in_=n[rt][:, cols], func=ACT.Tanh)

        def mix_multiply(rt, cols):
            nc.vector.tensor_mul(out=new_h[rt][:, cols], in0=one_minus_z[rt][:, cols], in1=n[rt][:, cols])

        def mix_add(rt, cols):
            nc.vector.tensor_add(out=new_h[rt][:, cols], in0=new_h[rt][:, cols], in1=z_h[rt][:, cols])

        def smooth_and_store(number, rt, cols, width):
            out_ps = bank(number, [P, width], F32, "out_ps")
            nc.tensor.matmul(out_ps[:], lhsT=blend[:], rhs=new_h[rt][:, cols], start=True, stop=True)
            nc.scalar.copy(out=out_sb[rt][:, cols], in_=out_ps[:])
            nc.sync.dma_start(out=out[rt * P : (rt + 1) * P, cols], in_=out_sb[rt][:, cols])

        i_n = bank(2, [P, HID], F32, "i_n")
        for g in range(IN_GROUPS):
            mx_pass(i_n[:], g, 0, N_GATE, 0, HID, start=(g == 0), stop=(g == IN_GROUPS - 1))
        halves = [slice(0, HALF), slice(HALF, HID)]
        for cols in halves:
            make_n(0, cols, i_n[:, cols])
        fillers = [(mix_multiply, halves[0]), (mix_add, halves[0]), (mix_multiply, halves[1]), (mix_add, halves[1])]

        quarters = [slice(q * QUARTER, (q + 1) * QUARTER) for q in range(HID // QUARTER)]
        quarter_banks = [3, 0, 1, 5]
        out_banks = [6, 7, 4]
        for q, cols in enumerate(quarters):
            i_n = bank(quarter_banks[q], [P, QUARTER], F32, "i_n_quarter")
            for g in range(IN_GROUPS):
                mx_pass(i_n[:], g, 1, N_GATE, q * QUARTER, QUARTER, start=(g == 0), stop=(g == IN_GROUPS - 1))
            make_n(1, cols, i_n[:])
            step, filler_cols = fillers[q]
            step(0, filler_cols)
            mix_multiply(1, cols)
            mix_add(1, cols)
            if q > 1:
                smooth_and_store(out_banks[q - 2], 1, quarters[q - 2], QUARTER)
        smooth_and_store(out_banks[2], 1, quarters[2], QUARTER)
        smooth_and_store(2, 0, halves[0], HALF)
        smooth_and_store(3, 0, halves[1], HALF)
        smooth_and_store(0, 1, quarters[3], QUARTER)
